import numpy as np
import ml_dtypes


def mxq(x, axis, fmt="e4m3"):
    dtype, down = {"e4m3": (ml_dtypes.float8_e4m3fn, 7), "e5m2": (ml_dtypes.float8_e5m2, 14)}[fmt]
    v = np.moveaxis(np.asarray(x, np.float32).astype(ml_dtypes.bfloat16).astype(np.float64), axis, -1)
    blocks = v.reshape(v.shape[:-1] + (-1, 32))
    amax = np.abs(blocks).max(-1, keepdims=True)
    byte = np.maximum(np.where(amax > 0, np.frexp(amax)[1] - 1 + 127, 0) - down, 1)
    scale = np.exp2(byte - 127.0)
    codes = (blocks / scale).astype(np.float32).astype(dtype).astype(np.float64)
    return np.moveaxis((codes * scale).reshape(v.shape), -1, axis)


WIDE = False


def mx_kscale(k):
    if not WIDE:
        return np.ones(k)
    levels = np.array([10, -10, 5, -5, 0])
    a = np.random.permutation(np.resize(levels, k // 512 * 4)).reshape(k // 512, 4)
    idx = np.arange(k)
    return np.exp2(a[idx // 512, idx % 128 // 32])


BF16 = ml_dtypes.bfloat16


def bf(x):
    return np.asarray(x, np.float32).astype(BF16)


def f64(x):
    return np.asarray(x).astype(np.float64)


E2M1 = np.array([0.0, 0.5, 1.0, 1.5, 2.0, 3.0, 4.0, 6.0, -0.0, -0.5, -1.0, -1.5, -2.0, -3.0, -4.0, -6.0])


def pack_weight(w, fmt):
    k, n = w.shape
    w = f64(bf(w)).reshape(k // 32, 32, n)
    amax = np.abs(w).max(1)
    if fmt == "e4m3":
        byte = np.frexp(amax)[1] - 1 + 127 - 7
    else:
        mant, ex = np.frexp(amax / 6.0)
        byte = np.where(mant > 0.5, ex, ex - 1) + 127
    byte = np.clip(np.where(amax > 0, byte, 1), 1, 254)
    scaled = (w * np.exp2(127.0 - byte)[:, None, :]).reshape(k, n).astype(np.float32)
    by_word = np.ascontiguousarray(scaled.reshape(k // 512, 128, 4, n).transpose(0, 1, 3, 2))
    if fmt == "e4m3":
        words = by_word.astype(ml_dtypes.float8_e4m3fn).view(np.uint8)
    else:
        c = by_word.astype(ml_dtypes.float4_e2m1fn).view(np.uint8) & 0xF
        words = c[..., 0::2] | (c[..., 1::2] << 4)
    return np.ascontiguousarray(words), np.ascontiguousarray(byte.astype(np.uint8).reshape(k // 512, 16, n))


def unpack_weight(words, scales, fmt):
    g, p, n, _ = words.shape
    if fmt == "e4m3":
        vals = np.ascontiguousarray(words).view(ml_dtypes.float8_e4m3fn).astype(np.float64)
    else:
        nib = np.empty((g, p, n, 4), np.uint8)
        nib[..., 0::2] = words & 0xF
        nib[..., 1::2] = words >> 4
        vals = E2M1[nib]
    vals = vals * np.repeat(np.exp2(scales.astype(np.float64) - 127.0), 8, axis=1)[..., None]
    return vals.transpose(0, 1, 3, 2).reshape(g * 512, n)


B, G, M, S, H = 128, 2, 2, 2048, 2048
ALPHA = 1.1


def entmax(alpha, v):
    v = v - np.max(v, axis=-1, keepdims=True)
    e = np.exp(v)
    s = (np.sum(e ** alpha, axis=-1, keepdims=True) + 1e-5) ** (1.0 / alpha)
    return e / s


def layernorm(h, w, b):
    mu = np.mean(h, axis=-1, keepdims=True)
    var = np.mean((h - mu) ** 2, axis=-1, keepdims=True)
    return (h - mu) * (1.0 / np.sqrt(var + 1e-5)) * w + b


def sigmoid(v):
    return 1.0 / (1.0 + np.exp(-v))


def group_matmul(a, w):
    nb, ng, nm, ns = a.shape
    y = a.transpose(1, 0, 2, 3).reshape(ng, nb * nm, ns) @ w.transpose(0, 2, 1)
    return y.reshape(ng, nb, nm, w.shape[1]).transpose(1, 0, 2, 3)


def setup_inputs():
    k = mx_kscale(S)
    ws = 0.003 * S ** (1.0 / ALPHA - 0.5)
    x = bf(np.random.standard_normal((B, G * S)) * np.tile(k, G))
    W_masks = bf(np.random.standard_normal((G, M, S)))
    W1 = (np.random.standard_normal((G, H, S)) + 0.3) * ws / k
    W2 = (np.random.standard_normal((G, H, S)) + 0.3) * ws / k
    W1_words, W1_scales = pack_weight(W1.swapaxes(1, 2).reshape(-1, H), "e4m3")
    W2_words, W2_scales = pack_weight(W2.swapaxes(1, 2).reshape(-1, H), "e4m3")
    return {"x": x,
            "W_masks": W_masks,
            "W1_words": W1_words,
            "W1_scales": W1_scales,
            "W2_words": W2_words,
            "W2_scales": W2_scales,
            "ln1_w": bf(1.0 + 0.2 * np.random.standard_normal((G, H))),
            "ln1_b": bf(0.2 * np.random.standard_normal((G, H))),
            "ln2_w": bf(1.0 + 0.2 * np.random.standard_normal((G, H))),
            "ln2_b": bf(0.2 * np.random.standard_normal((G, H)))}


def reference(x, W_masks, W1_words, W1_scales, W2_words, W2_scales, ln1_w, ln1_b, ln2_w, ln2_b):
    g, m, s = W_masks.shape
    b = x.shape[0]
    xg = f64(x).reshape(b, g, s)
    mask = entmax(ALPHA, f64(W_masks))
    weighted = xg[:, :, None, :] * mask[None]
    wq = mxq(weighted, 3, "e4m3")
    h1 = group_matmul(wq, unpack_weight(W1_words, W1_scales, "e4m3").reshape(G, S, H).swapaxes(1, 2))
    h2 = group_matmul(wq, unpack_weight(W2_words, W2_scales, "e4m3").reshape(G, S, H).swapaxes(1, 2))
    n1 = layernorm(h1, f64(ln1_w)[None, :, None, :], f64(ln1_b)[None, :, None, :])
    n2 = layernorm(h2, f64(ln2_w)[None, :, None, :], f64(ln2_b)[None, :, None, :])
    activated = np.maximum(sigmoid(n1) * n2, 0.0)
    group_out = np.sum(activated, axis=2)
    return group_out.reshape(b, g * group_out.shape[-1])

@@ -1,0 +1,321 @@
+from contextlib import ExitStack
+
+import concourse.mybir as mybir
+from concourse.masks import make_identity
+
+F32 = mybir.dt.float32
+BF16 = mybir.dt.bfloat16
+I32 = mybir.dt.int32
+U32 = mybir.dt.uint32
+U8 = mybir.dt.uint8
+FP8X4 = mybir.dt.float8_e4m3fn_x4
+ALU = mybir.AluOpType
+ACT = mybir.ActivationFunctionType
+AX = mybir.AxisListType
+
+P = 128
+GROUPS = 2
+MASKS = 2
+S = 2048
+H = 2048
+PACK = 4
+K_PASS = P * PACK
+PASSES = S // K_PASS
+N_TILE = 512
+N_TILES = H // N_TILE
+ROWS = GROUPS * MASKS
+TAPS = PASSES * PACK
+ALPHA = 1.1
+EPS = 1e-5
+
+FLOPS = 2 * P * GROUPS * MASKS * S * H * 2
+
+
+def tile_dynamicfeaturegroupinglayer_w_e_kernel(
+    tc, x, W_masks, W1_words, W1_scales, W2_words, W2_scales, ln1_w, ln1_b, ln2_w, ln2_b, out
+):
+    nc = tc.nc
+    w_words = (W1_words, W2_words)
+    w_scales = (W1_scales, W2_scales)
+    ln_rows = (ln1_w, ln1_b, ln2_w, ln2_b)
+
+    with ExitStack() as ctx:
+        ctx.enter_context(tc.manual_schedule())
+        keep = ctx.enter_context(tc.tile_pool(name="keep", bufs=1))
+        small = ctx.enter_context(tc.tile_pool(name="small", bufs=4))
+        stage = ctx.enter_context(tc.tile_pool(name="stage", bufs=2))
+        wpool = ctx.enter_context(tc.tile_pool(name="wpool", bufs=8))
+        hpool = ctx.enter_context(tc.tile_pool(name="hpool", bufs=3))
+        tpool = ctx.enter_context(tc.tile_pool(name="tpool", bufs=6))
+        psum = ctx.enter_context(tc.psum_pool(name="psum", bufs=8))
+
+        planes = keep.tile([P, 2 * GROUPS, H], U8, align_bytes=64)
+        nc.vector.memset(planes[:].rearrange("p f n -> p (f n)").bitcast(I32), 0)
+        prm = keep.tile([P, H], BF16)
+        nc.vector.memset(prm[:].bitcast(I32), 0)
+        ones = keep.tile([P, P], F32)
+        nc.vector.memset(ones[:], 1.0)
+        eps_col = keep.tile([P, 1], F32)
+        nc.vector.memset(eps_col[:], EPS)
+        neg_half = keep.tile([P, 1], F32)
+        nc.vector.memset(neg_half[:], -0.5)
+        ident_f = keep.tile([P, P], F32)
+        make_identity(nc, ident_f[:])
+        ident_b = keep.tile([P, P], BF16)
+        make_identity(nc, ident_b[:])
+
+        wm = keep.tile([P, ROWS, TAPS], BF16)
+        nc.sync.dma_start(
+            out=wm[:].rearrange("p a (c t) -> p (a c) t", t=PACK),
+            in_=W_masks.rearrange("g m (c p t) -> p (g m c) t", c=PASSES, p=P, t=PACK),
+        )
+        x_sb = keep.tile([P, GROUPS * S], BF16)
+        nc.sync.dma_start(out=x_sb[:], in_=x)
+        for r in range(4):
+            nc.scalar.dma_start(out=prm[2 * r : 2 * r + 2, :], in_=ln_rows[r])
+
+        def load_scales(g, v):
+            for q in range(4):
+                nc.sync.dma_start(
+                    out=planes[32 * q : 32 * q + 16, 2 * g + v, :].bitcast(I32),
+                    in_=w_scales[v][PASSES * g : PASSES * (g + 1), 4 * q : 4 * q + 4, :].bitcast(I32),
+                )
+
+        def load_words(g, v):
+            chunks = []
+            for c in range(PASSES):
+                chunk = wpool.tile([P, H], U32, name="chunk", align_bytes=64)
+                nc.sync.dma_start(
+                    out=chunk[:].bitcast(I32),
+                    in_=w_words[v][PASSES * g + c].rearrange("p n t -> p (n t)").bitcast(I32),
+                )
+                chunks.append(chunk)
+            return chunks
+
+        phases = [(g, v) for g in range(GROUPS) for v in range(2)]
+        loaded = {}
+        load_scales(0, 0)
+        loaded[(0, 0)] = load_words(0, 0)
+        for g, v in phases[1:]:
+            load_scales(g, v)
+        loaded[(0, 1)] = load_words(0, 1)
+
+        spread = keep.tile([P, 8, H], BF16)
+
+        def spread_matmuls(g, v):
+            wides = []
+            for r in (4 * v + g, 4 * v + 2 + g):
+                for half in range(2):
+                    wide = psum.tile([P, 2 * N_TILE], BF16, name="wide", tag="bank")
+                    for j in range(2):
+                        first = (2 * half + j) * N_TILE
+                        nc.tensor.matmul(
+                            out=wide[:, j * N_TILE : (j + 1) * N_TILE],
+                            lhsT=ident_b[:, r : r + 1].to_broadcast([P, P]),
+                            rhs=prm[:, first : first + N_TILE],
+                            start=True,
+                            stop=True,
+                        )
+                    wides.append((r, half, wide))
+            return wides
+
+        def spread_copies(wides):
+            for r, half, wide in wides:
+                nc.scalar.copy(out=spread[:, r, 2 * half * N_TILE : 2 * (half + 1) * N_TILE], in_=wide[:])
+
+        a_codes = keep.tile([P, GROUPS * PASSES, MASKS * P], U32, align_bytes=64)
+        a_scales = keep.tile([P, GROUPS * PASSES, MASKS * P], U8, align_bytes=64)
+        x_words = x_sb[:].bitcast(F32)
+        mask = keep.tile([P, ROWS, TAPS], F32)
+
+        def transpose_group(g):
+            banks = []
+            for pair in range(PASSES // 2):
+                xt = psum.tile([P, 2, 2, P], F32, name="xt", tag="bank")
+                for i in range(2):
+                    gp = PASSES * g + 2 * pair + i
+                    for u in range(2):
+                        nc.tensor.transpose(
+                            xt[:, i, u, :], x_words[:, 256 * gp + u : 256 * (gp + 1) : 2], ident_f[:]
+                        )
+                banks.append(xt)
+            return banks
+
+        def quantise_group(g, banks):
+            previous = None
+            for c in range(PASSES):
+                grouped = stage.tile([P, MASKS, P, PACK], BF16, name="grouped", align_bytes=64)
+                for m in range(MASKS):
+                    nc.vector.tensor_tensor(
+                        out=grouped[:, m].rearrange("p b (u e) -> p b u e", e=2),
+                        in0=banks[c // 2][:, c % 2].bitcast(BF16).rearrange("p u (b e) -> p b u e", e=2),
+                        in1=mask[:, MASKS * g + m, PACK * c : PACK * (c + 1)]
+                        .rearrange("p (u e) -> p u e", e=2)
+                        .unsqueeze(1)
+                        .to_broadcast([P, P, 2, 2]),
+                        op=ALU.mult,
+                    )
+                if previous is not None:
+                    quantise(g, c - 1, previous)
+                previous = grouped
+            quantise(g, PASSES - 1, previous)
+
+        def quantise(g, c, grouped):
+            nc.vector.quantize_mx(
+                out=a_codes[:, PASSES * g + c, :].bitcast(FP8X4),
+                scales=a_scales[:, PASSES * g + c, :],
+                in_=grouped[:].rearrange("p m b t -> p (m b t)"),
+            )
+
+        own_top = small.tile([P, ROWS], F32)
+        nc.vector.tensor_reduce(out=own_top[:], in_=wm[:], axis=AX.X, op=ALU.max)
+        tops = psum.tile([P, ROWS, P], F32, tag="bank")
+        for a in range(ROWS):
+            nc.tensor.transpose(tops[:, a, :], own_top[:, a : a + 1].to_broadcast([P, P]), ident_f[:])
+        neg_top = small.tile([P, ROWS], F32)
+        nc.vector.tensor_reduce(out=neg_top[:], in_=tops[:], axis=AX.X, op=ALU.max, negate=True)
+        neg_top_alpha = small.tile([P, ROWS], F32)
+        nc.vector.tensor_scalar_mul(out=neg_top_alpha[:], in0=neg_top[:], scalar1=ALPHA)
+        x_banks = transpose_group(0)
+        powered = small.tile([P, ROWS, TAPS], F32)
+        part = small.tile([P, ROWS], F32)
+        for a in range(ROWS):
+            nc.scalar.activation(
+                out=powered[:, a, :],
+                in_=wm[:, a, :],
+                func=ACT.Exp,
+                scale=ALPHA,
+                bias=neg_top_alpha[:, a : a + 1],
+                accum_out=part[:, a : a + 1],
+            )
+        total = psum.tile([P, ROWS], F32, tag="bank")
+        nc.tensor.matmul(out=total[:], lhsT=ones[:], rhs=part[:], start=True, stop=True)
+        log_total = small.tile([P, ROWS], F32)
+        nc.scalar.activation(out=log_total[:], in_=total[:], func=ACT.Ln, bias=eps_col[:, 0:1])
+        shift = small.tile([P, ROWS], F32)
+        nc.vector.scalar_tensor_tensor(
+            out=shift[:], in0=log_total[:], scalar=-1.0 / ALPHA, in1=neg_top[:], op0=ALU.mult, op1=ALU.add
+        )
+        for a in range(ROWS):
+            nc.scalar.activation(out=mask[:, a, :], in_=wm[:, a, :], func=ACT.Exp, bias=shift[:, a : a + 1])
+        first_rows = spread_matmuls(0, 0)
+        warm = small.tile([P, 1], F32)
+        nc.scalar.activation(out=warm[:], in_=eps_col[:], func=ACT.Sigmoid)
+        spread_copies(first_rows)
+        quantise_group(0, x_banks)
+
+        units = [(g, v, m) for g in range(GROUPS) for v in range(2) for m in range(MASKS)]
+        n_units = len(units)
+        banks_of, h_of, neg_mean_of, rstd_of, t_of = {}, {}, {}, {}, {}
+
+        def products(i):
+            g, v, m = units[i]
+            banks = []
+            for n in range(N_TILES):
+                acc = psum.tile([P, N_TILE], F32, name="acc", tag="bank")
+                banks.append(acc)
+            for c in range(PASSES):
+                gp = PASSES * g + c
+                for n in range(N_TILES):
+                    cols = slice(n * N_TILE, (n + 1) * N_TILE)
+                    nc.tensor.matmul_mx(
+                        out=banks[n][:],
+                        lhsT=a_codes[:, gp, m * P : (m + 1) * P].bitcast(FP8X4),
+                        lhsT_scale=a_scales[:, gp, m * P : (m + 1) * P],
+                        rhs=loaded[(g, v)][c][:, cols].bitcast(FP8X4),
+                        rhs_scale=planes[4 * c : P, 2 * g + v, cols],
+                        start=(c == 0),
+                        stop=(c == PASSES - 1),
+                    )
+            banks_of[i] = banks
+
+        def leave_psum(i):
+            h = hpool.tile([P, H], F32, name="h")
+            sums = small.tile([P, N_TILES], F32, name="sums")
+            for n in range(N_TILES):
+                nc.scalar.activation(
+                    out=h[:, n * N_TILE : (n + 1) * N_TILE],
+                    in_=banks_of[i][n][:],
+                    func=ACT.Copy,
+                    accum_out=sums[:, n : n + 1],
+                )
+            scaled = small.tile([P, N_TILES], F32, name="scaled")
+            neg_mean = small.tile([P, 1], F32, name="neg_mean")
+            nc.scalar.activation(out=scaled[:], in_=sums[:], func=ACT.Copy, scale=-1.0 / H, accum_out=neg_mean[:])
+            h_of[i] = h
+            neg_mean_of[i] = neg_mean
+
+        def spread_of_row(i):
+            squares = stage.tile([P, H], BF16, name="squares")
+            sum_sq = small.tile([P, 1], F32, name="sum_sq")
+            nc.scalar.activation(
+                out=squares[:], in_=h_of[i][:], func=ACT.Square, bias=neg_mean_of[i][:, 0:1], accum_out=sum_sq[:]
+            )
+            var_eps = small.tile([P, 1], F32, name="var_eps")
+            nc.gpsimd.tensor_scalar(
+                out=var_eps[:], in0=sum_sq[:], scalar1=1.0 / H, scalar2=EPS, op0=ALU.mult, op1=ALU.add
+            )
+            rstd = small.tile([P, 1], F32, name="rstd")
+            nc.gpsimd.tensor_tensor(out=rstd[:], in0=var_eps[:], in1=neg_half[:], op=ALU.pow)
+            rstd_of[i] = rstd
+
+        def centre_and_gain(i):
+            g, v, m = units[i]
+            t = tpool.tile([P, H], F32, name="t")
+            nc.vector.scalar_tensor_tensor(
+                out=t[:],
+                in0=h_of[i][:],
+                scalar=neg_mean_of[i][:, 0:1],
+                in1=spread[:, 4 * v + g, :],
+                op0=ALU.add,
+                op1=ALU.mult,
+            )
+            t_of[i] = t
+
+        def scale_and_bias(i):
+            g, v, m = units[i]
+            nc.vector.scalar_tensor_tensor(
+                out=t_of[i][:],
+                in0=t_of[i][:],
+                scalar=rstd_of[i][:, 0:1],
+                in1=spread[:, 4 * v + 2 + g, :],
+                op0=ALU.mult,
+                op1=ALU.add,
+            )
+
+        for step in range(n_units + 1):
+            if step < n_units:
+                g, v, m = units[step]
+                products(step)
+                if m == MASKS - 1 and step // MASKS + 2 < len(phases):
+                    loaded[phases[step // MASKS + 2]] = load_words(*phases[step // MASKS + 2])
+                if step == 0:
+                    quantise_group(1, transpose_group(1))
+                if 0 < step < len(phases):
+                    rows = spread_matmuls(*phases[step])
+                leave_psum(step)
+            k = step - 3
+            if k >= 0 and units[k][1] == 0:
+                nc.scalar.activation(out=t_of[k][:], in_=t_of[k][:], func=ACT.Sigmoid)
+            if step < n_units:
+                spread_of_row(step)
+                if 0 < step < len(phases):
+                    spread_copies(rows)
+                centre_and_gain(step)
+            j = step - 1
+            if j >= 0:
+                g, v, m = units[j]
+                scale_and_bias(j)
+                if v == 1:
+                    nc.vector.scalar_tensor_tensor(
+                        out=t_of[j][:], in0=t_of[j][:], scalar=0.0, in1=t_of[j - MASKS][:], op0=ALU.max, op1=ALU.mult
+                    )
+                    if m == MASKS - 1:
+                        for n in range(N_TILES):
+                            cols = slice(n * N_TILE, (n + 1) * N_TILE)
+                            nc.vector.tensor_tensor(
+                                out=t_of[j - 1][:, cols], in0=t_of[j - 1][:, cols], in1=t_of[j][:, cols], op=ALU.add
+                            )
+                            nc.sync.dma_start(
+                                out=out[:, g * H + n * N_TILE : g * H + (n + 1) * N_TILE], in_=t_of[j - 1][:, cols]
+                            )

@@ -27,6 +27,8 @@ ROWS = GROUPS * MASKS
 TAPS = PASSES * PACK
 ALPHA = 1.1
 EPS = 1e-5
+EXPONENT_COARSE = -29.0 / 32.0
+EXPONENT_REST = -1.0 / ALPHA - EXPONENT_COARSE
 
 FLOPS = 2 * P * GROUPS * MASKS * S * H * 2
 
@@ -55,8 +57,9 @@ def tile_dynamicfeaturegroupinglayer_w_e_kernel(
         nc.vector.memset(prm[:].bitcast(I32), 0)
         ones = keep.tile([P, P], F32)
         nc.vector.memset(ones[:], 1.0)
-        eps_col = keep.tile([P, 1], F32)
-        nc.vector.memset(eps_col[:], EPS)
+        exponents = keep.tile([P, 2, ROWS], F32)
+        nc.vector.memset(exponents[:, 0, :], EXPONENT_COARSE)
+        nc.vector.memset(exponents[:, 1, :], EXPONENT_REST)
         neg_half = keep.tile([P, 1], F32)
         nc.vector.memset(neg_half[:], -0.5)
         ident_f = keep.tile([P, P], F32)
@@ -119,9 +122,13 @@ def tile_dynamicfeaturegroupinglayer_w_e_kernel(
                     wides.append((r, half, wide))
             return wides
 
-        def spread_copies(wides):
+        def spread_copies(wides, share):
             for r, half, wide in wides:
-                nc.scalar.copy(out=spread[:, r, 2 * half * N_TILE : 2 * (half + 1) * N_TILE], in_=wide[:])
+                target = spread[:, r, 2 * half * N_TILE : 2 * (half + 1) * N_TILE]
+                if share and half == 1:
+                    nc.vector.tensor_copy(out=target, in_=wide[:])
+                else:
+                    nc.scalar.copy(out=target, in_=wide[:])
 
         a_codes = keep.tile([P, GROUPS * PASSES, MASKS * P], U32, align_bytes=64)
         a_scales = keep.tile([P, GROUPS * PASSES, MASKS * P], U8, align_bytes=64)
@@ -176,7 +183,6 @@ def tile_dynamicfeaturegroupinglayer_w_e_kernel(
         nc.vector.tensor_reduce(out=neg_top[:], in_=tops[:], axis=AX.X, op=ALU.max, negate=True)
         neg_top_alpha = small.tile([P, ROWS], F32)
         nc.vector.tensor_scalar_mul(out=neg_top_alpha[:], in0=neg_top[:], scalar1=ALPHA)
-        x_banks = transpose_group(0)
         powered = small.tile([P, ROWS, TAPS], F32)
         part = small.tile([P, ROWS], F32)
         for a in range(ROWS):
@@ -188,20 +194,27 @@ def tile_dynamicfeaturegroupinglayer_w_e_kernel(
                 bias=neg_top_alpha[:, a : a + 1],
                 accum_out=part[:, a : a + 1],
             )
-        total = psum.tile([P, ROWS], F32, tag="bank")
-        nc.tensor.matmul(out=total[:], lhsT=ones[:], rhs=part[:], start=True, stop=True)
-        log_total = small.tile([P, ROWS], F32)
-        nc.scalar.activation(out=log_total[:], in_=total[:], func=ACT.Ln, bias=eps_col[:, 0:1])
-        shift = small.tile([P, ROWS], F32)
-        nc.vector.scalar_tensor_tensor(
-            out=shift[:], in0=log_total[:], scalar=-1.0 / ALPHA, in1=neg_top[:], op0=ALU.mult, op1=ALU.add
-        )
+        total_ps = psum.tile([P, ROWS], F32, tag="bank")
+        nc.tensor.matmul(out=total_ps[:], lhsT=ones[:], rhs=part[:], start=True, stop=True)
+        e = small.tile([P, ROWS, TAPS], F32)
         for a in range(ROWS):
-            nc.scalar.activation(out=mask[:, a, :], in_=wm[:, a, :], func=ACT.Exp, bias=shift[:, a : a + 1])
-        first_rows = spread_matmuls(0, 0)
+            nc.scalar.activation(out=e[:, a, :], in_=wm[:, a, :], func=ACT.Exp, bias=neg_top[:, a : a + 1])
+        total = small.tile([P, ROWS], F32)
+        nc.vector.tensor_scalar_add(out=total[:], in0=total_ps[:], scalar1=EPS)
+        factors = small.tile([P, 2, ROWS], F32)
+        nc.gpsimd.tensor_tensor(
+            out=factors[:], in0=total[:].unsqueeze(1).to_broadcast([P, 2, ROWS]), in1=exponents[:], op=ALU.pow
+        )
+        inv_norm = small.tile([P, ROWS], F32)
+        nc.vector.tensor_tensor(out=inv_norm[:], in0=factors[:, 0, :], in1=factors[:, 1, :], op=ALU.mult)
+        nc.vector.tensor_tensor(
+            out=mask[:], in0=e[:], in1=inv_norm[:].unsqueeze(2).to_broadcast([P, ROWS, TAPS]), op=ALU.mult
+        )
+        x_banks = transpose_group(0)
         warm = small.tile([P, 1], F32)
-        nc.scalar.activation(out=warm[:], in_=eps_col[:], func=ACT.Sigmoid)
-        spread_copies(first_rows)
+        nc.scalar.activation(out=warm[:], in_=neg_half[:], func=ACT.Sigmoid)
+        for v in range(2):
+            spread_copies(spread_matmuls(0, v), False)
         quantise_group(0, x_banks)
 
         units = [(g, v, m) for g in range(GROUPS) for v in range(2) for m in range(MASKS)]
@@ -291,16 +304,16 @@ def tile_dynamicfeaturegroupinglayer_w_e_kernel(
                     loaded[phases[step // MASKS + 2]] = load_words(*phases[step // MASKS + 2])
                 if step == 0:
                     quantise_group(1, transpose_group(1))
-                if 0 < step < len(phases):
-                    rows = spread_matmuls(*phases[step])
+                if step in (1, 2):
+                    rows = spread_matmuls(1, step - 1)
                 leave_psum(step)
             k = step - 3
             if k >= 0 and units[k][1] == 0:
                 nc.scalar.activation(out=t_of[k][:], in_=t_of[k][:], func=ACT.Sigmoid)
             if step < n_units:
                 spread_of_row(step)
-                if 0 < step < len(phases):
-                    spread_copies(rows)
+                if step in (1, 2):
+                    spread_copies(rows, True)
                 centre_and_gain(step)
             j = step - 1
             if j >= 0:

@@ -23,6 +23,8 @@ K_PASS = P * PACK
 PASSES = S // K_PASS
 N_TILE = 512
 N_TILES = H // N_TILE
+J_TILES = H // P
+J_BANK = N_TILE // P
 ROWS = GROUPS * MASKS
 TAPS = PASSES * PACK
 ALPHA = 1.1
@@ -45,16 +47,15 @@ def tile_dynamicfeaturegroupinglayer_w_e_kernel(
         ctx.enter_context(tc.manual_schedule())
         keep = ctx.enter_context(tc.tile_pool(name="keep", bufs=1))
         small = ctx.enter_context(tc.tile_pool(name="small", bufs=4))
-        stage = ctx.enter_context(tc.tile_pool(name="stage", bufs=2))
-        wpool = ctx.enter_context(tc.tile_pool(name="wpool", bufs=8))
-        hpool = ctx.enter_context(tc.tile_pool(name="hpool", bufs=3))
-        tpool = ctx.enter_context(tc.tile_pool(name="tpool", bufs=6))
-        psum = ctx.enter_context(tc.psum_pool(name="psum", bufs=8))
+        stage = ctx.enter_context(tc.tile_pool(name="stage", bufs=4))
+        wpool = ctx.enter_context(tc.tile_pool(name="wpool", bufs=12))
+        zpool = ctx.enter_context(tc.tile_pool(name="zpool", bufs=3))
+        gpool = ctx.enter_context(tc.tile_pool(name="gpool", bufs=2))
+        psx = ctx.enter_context(tc.psum_pool(name="psx", bufs=4))
+        psy = ctx.enter_context(tc.psum_pool(name="psy", bufs=4))
 
         planes = keep.tile([P, 2 * GROUPS, H], U8, align_bytes=64)
         nc.vector.memset(planes[:].rearrange("p f n -> p (f n)").bitcast(I32), 0)
-        prm = keep.tile([P, H], BF16)
-        nc.vector.memset(prm[:].bitcast(I32), 0)
         ones = keep.tile([P, P], F32)
         nc.vector.memset(ones[:], 1.0)
         exponents = keep.tile([P, 2, ROWS], F32)
@@ -74,8 +75,11 @@ def tile_dynamicfeaturegroupinglayer_w_e_kernel(
         )
         x_sb = keep.tile([P, GROUPS * S], BF16)
         nc.sync.dma_start(out=x_sb[:], in_=x)
+        prm = keep.tile([P, P], BF16)
         for r in range(4):
-            nc.scalar.dma_start(out=prm[2 * r : 2 * r + 2, :], in_=ln_rows[r])
+            nc.scalar.dma_start(
+                out=prm[32 * r : 32 * (r + 1), :], in_=ln_rows[r].rearrange("g (jt p) -> (g jt) p", p=P)
+            )
 
         def load_scales(g, v):
             for q in range(4):
@@ -102,43 +106,17 @@ def tile_dynamicfeaturegroupinglayer_w_e_kernel(
         for g, v in phases[1:]:
             load_scales(g, v)
         loaded[(0, 1)] = load_words(0, 1)
-
-        spread = keep.tile([P, 8, H], BF16)
-
-        def spread_matmuls(g, v):
-            wides = []
-            for r in (4 * v + g, 4 * v + 2 + g):
-                for half in range(2):
-                    wide = psum.tile([P, 2 * N_TILE], BF16, name="wide", tag="bank")
-                    for j in range(2):
-                        first = (2 * half + j) * N_TILE
-                        nc.tensor.matmul(
-                            out=wide[:, j * N_TILE : (j + 1) * N_TILE],
-                            lhsT=ident_b[:, r : r + 1].to_broadcast([P, P]),
-                            rhs=prm[:, first : first + N_TILE],
-                            start=True,
-                            stop=True,
-                        )
-                    wides.append((r, half, wide))
-            return wides
-
-        def spread_copies(wides, share):
-            for r, half, wide in wides:
-                target = spread[:, r, 2 * half * N_TILE : 2 * (half + 1) * N_TILE]
-                if share and half == 1:
-                    nc.vector.tensor_copy(out=target, in_=wide[:])
-                else:
-                    nc.scalar.copy(out=target, in_=wide[:])
+        loaded[(1, 0)] = load_words(1, 0)
 
         a_codes = keep.tile([P, GROUPS * PASSES, MASKS * P], U32, align_bytes=64)
         a_scales = keep.tile([P, GROUPS * PASSES, MASKS * P], U8, align_bytes=64)
         x_words = x_sb[:].bitcast(F32)
         mask = keep.tile([P, ROWS, TAPS], F32)
 
-        def transpose_group(g):
+        def transpose_group(g, pool):
             banks = []
             for pair in range(PASSES // 2):
-                xt = psum.tile([P, 2, 2, P], F32, name="xt", tag="bank")
+                xt = pool.tile([P, 2, 2, P], F32, name="xt", tag="bank")
                 for i in range(2):
                     gp = PASSES * g + 2 * pair + i
                     for u in range(2):
@@ -148,35 +126,29 @@ def tile_dynamicfeaturegroupinglayer_w_e_kernel(
                 banks.append(xt)
             return banks
 
-        def quantise_group(g, banks):
-            previous = None
-            for c in range(PASSES):
-                grouped = stage.tile([P, MASKS, P, PACK], BF16, name="grouped", align_bytes=64)
-                for m in range(MASKS):
-                    nc.vector.tensor_tensor(
-                        out=grouped[:, m].rearrange("p b (u e) -> p b u e", e=2),
-                        in0=banks[c // 2][:, c % 2].bitcast(BF16).rearrange("p u (b e) -> p b u e", e=2),
-                        in1=mask[:, MASKS * g + m, PACK * c : PACK * (c + 1)]
-                        .rearrange("p (u e) -> p u e", e=2)
-                        .unsqueeze(1)
-                        .to_broadcast([P, P, 2, 2]),
-                        op=ALU.mult,
-                    )
-                if previous is not None:
-                    quantise(g, c - 1, previous)
-                previous = grouped
-            quantise(g, PASSES - 1, previous)
+        def weigh(g, c, m, words):
+            grouped = stage.tile([P, P, PACK], BF16, name="grouped", align_bytes=64)
+            nc.vector.tensor_tensor(
+                out=grouped[:].rearrange("p b (u e) -> p b u e", e=2),
+                in0=words.bitcast(BF16).rearrange("p u (b e) -> p b u e", e=2),
+                in1=mask[:, MASKS * g + m, PACK * c : PACK * (c + 1)]
+                .rearrange("p (u e) -> p u e", e=2)
+                .unsqueeze(1)
+                .to_broadcast([P, P, 2, 2]),
+                op=ALU.mult,
+            )
+            return grouped
 
-        def quantise(g, c, grouped):
+        def quantise(g, c, m, grouped):
             nc.vector.quantize_mx(
-                out=a_codes[:, PASSES * g + c, :].bitcast(FP8X4),
-                scales=a_scales[:, PASSES * g + c, :],
-                in_=grouped[:].rearrange("p m b t -> p (m b t)"),
+                out=a_codes[:, PASSES * g + c, m * P : (m + 1) * P].bitcast(FP8X4),
+                scales=a_scales[:, PASSES * g + c, m * P : (m + 1) * P],
+                in_=grouped[:].rearrange("p b t -> p (b t)"),
             )
 
         own_top = small.tile([P, ROWS], F32)
         nc.vector.tensor_reduce(out=own_top[:], in_=wm[:], axis=AX.X, op=ALU.max)
-        tops = psum.tile([P, ROWS, P], F32, tag="bank")
+        tops = psx.tile([P, ROWS, P], F32, tag="bank")
         for a in range(ROWS):
             nc.tensor.transpose(tops[:, a, :], own_top[:, a : a + 1].to_broadcast([P, P]), ident_f[:])
         neg_top = small.tile([P, ROWS], F32)
@@ -194,7 +166,7 @@ def tile_dynamicfeaturegroupinglayer_w_e_kernel(
                 bias=neg_top_alpha[:, a : a + 1],
                 accum_out=part[:, a : a + 1],
             )
-        total_ps = psum.tile([P, ROWS], F32, tag="bank")
+        total_ps = psx.tile([P, ROWS], F32, tag="bank")
         nc.tensor.matmul(out=total_ps[:], lhsT=ones[:], rhs=part[:], start=True, stop=True)
         e = small.tile([P, ROWS, TAPS], F32)
         for a in range(ROWS):
@@ -210,125 +182,196 @@ def tile_dynamicfeaturegroupinglayer_w_e_kernel(
         nc.vector.tensor_tensor(
             out=mask[:], in0=e[:], in1=inv_norm[:].unsqueeze(2).to_broadcast([P, ROWS, TAPS]), op=ALU.mult
         )
-        x_banks = transpose_group(0)
+        x0_banks = transpose_group(0, psy)
+        prm_ps = psx.tile([P, P], BF16, tag="bank")
+        nc.tensor.transpose(prm_ps[:], prm[:], ident_b[:])
         warm = small.tile([P, 1], F32)
         nc.scalar.activation(out=warm[:], in_=neg_half[:], func=ACT.Sigmoid)
-        for v in range(2):
-            spread_copies(spread_matmuls(0, v), False)
-        quantise_group(0, x_banks)
+        prm_t = keep.tile([P, P], F32)
+        nc.scalar.copy(out=prm_t[:], in_=prm_ps[:])
+        x1_words = keep.tile([P, PASSES, 2, P], F32)
 
         units = [(g, v, m) for g in range(GROUPS) for v in range(2) for m in range(MASKS)]
         n_units = len(units)
-        banks_of, h_of, neg_mean_of, rstd_of, t_of = {}, {}, {}, {}, {}
+        banks_of, mv_of, rstd_of, z_of, zt_of, gate_of, stats_of = {}, {}, {}, {}, {}, {}, {}
 
-        def products(i):
-            g, v, m = units[i]
-            banks = []
-            for n in range(N_TILES):
-                acc = psum.tile([P, N_TILE], F32, name="acc", tag="bank")
-                banks.append(acc)
-            for c in range(PASSES):
-                gp = PASSES * g + c
+        def one_pass(u, c, n):
+            g, v, m = units[u]
+            gp = PASSES * g + c
+            cols = slice(n * N_TILE, (n + 1) * N_TILE)
+            nc.tensor.matmul_mx(
+                out=banks_of[u][n][:],
+                lhsT=a_codes[:, gp, m * P : (m + 1) * P].bitcast(FP8X4),
+                lhsT_scale=a_scales[:, gp, m * P : (m + 1) * P],
+                rhs=loaded[(g, v)][c][:, cols].bitcast(FP8X4),
+                rhs_scale=planes[4 * c : P, 2 * g + v, cols],
+                start=(c == 0),
+                stop=(c == PASSES - 1),
+            )
+
+        def products(u, pool, bank_by_bank):
+            banks_of[u] = []
+            if bank_by_bank:
                 for n in range(N_TILES):
-                    cols = slice(n * N_TILE, (n + 1) * N_TILE)
-                    nc.tensor.matmul_mx(
-                        out=banks[n][:],
-                        lhsT=a_codes[:, gp, m * P : (m + 1) * P].bitcast(FP8X4),
-                        lhsT_scale=a_scales[:, gp, m * P : (m + 1) * P],
-                        rhs=loaded[(g, v)][c][:, cols].bitcast(FP8X4),
-                        rhs_scale=planes[4 * c : P, 2 * g + v, cols],
-                        start=(c == 0),
-                        stop=(c == PASSES - 1),
-                    )
-            banks_of[i] = banks
+                    acc = pool.tile([P, N_TILE], F32, name="acc", tag="bank")
+                    banks_of[u].append(acc)
+                    for c in range(PASSES):
+                        one_pass(u, c, n)
+            else:
+                for n in range(N_TILES):
+                    acc = pool.tile([P, N_TILE], F32, name="acc", tag="bank")
+                    banks_of[u].append(acc)
+                for c in range(PASSES):
+                    for n in range(N_TILES):
+                        one_pass(u, c, n)
 
-        def leave_psum(i):
-            h = hpool.tile([P, H], F32, name="h")
-            sums = small.tile([P, N_TILES], F32, name="sums")
-            for n in range(N_TILES):
-                nc.scalar.activation(
-                    out=h[:, n * N_TILE : (n + 1) * N_TILE],
-                    in_=banks_of[i][n][:],
-                    func=ACT.Copy,
-                    accum_out=sums[:, n : n + 1],
-                )
-            scaled = small.tile([P, N_TILES], F32, name="scaled")
-            neg_mean = small.tile([P, 1], F32, name="neg_mean")
-            nc.scalar.activation(out=scaled[:], in_=sums[:], func=ACT.Copy, scale=-1.0 / H, accum_out=neg_mean[:])
-            h_of[i] = h
-            neg_mean_of[i] = neg_mean
+        def leave_psum(u, n):
+            if n == 0:
+                z = zpool.tile([P, H], F32, name="z")
+                z_of[u] = z
+            nc.scalar.copy(out=z_of[u][:, n * N_TILE : (n + 1) * N_TILE], in_=banks_of[u][n][:])
 
-        def spread_of_row(i):
-            squares = stage.tile([P, H], BF16, name="squares")
-            sum_sq = small.tile([P, 1], F32, name="sum_sq")
-            nc.scalar.activation(
-                out=squares[:], in_=h_of[i][:], func=ACT.Square, bias=neg_mean_of[i][:, 0:1], accum_out=sum_sq[:]
-            )
+        def bank_stats(u, n):
+            if n == 0:
+                stats = small.tile([P, N_TILES, 6], F32, name="stats")
+                stats_of[u] = stats
+            nc.vector.bn_stats(out=stats_of[u][:, n, :], in_=z_of[u][:, n * N_TILE : (n + 1) * N_TILE])
+
+        def row_stats(u):
+            mv = small.tile([P, 2], F32, name="mv")
+            nc.vector.bn_aggr(out=mv[:], in_=stats_of[u][:].rearrange("p n s -> p (n s)"))
             var_eps = small.tile([P, 1], F32, name="var_eps")
-            nc.gpsimd.tensor_scalar(
-                out=var_eps[:], in0=sum_sq[:], scalar1=1.0 / H, scalar2=EPS, op0=ALU.mult, op1=ALU.add
-            )
+            nc.vector.tensor_scalar_add(out=var_eps[:], in0=mv[:, 1:2], scalar1=EPS)
             rstd = small.tile([P, 1], F32, name="rstd")
             nc.gpsimd.tensor_tensor(out=rstd[:], in0=var_eps[:], in1=neg_half[:], op=ALU.pow)
-            rstd_of[i] = rstd
+            mv_of[u], rstd_of[u] = mv, rstd
 
-        def centre_and_gain(i):
-            g, v, m = units[i]
-            t = tpool.tile([P, H], F32, name="t")
-            nc.vector.scalar_tensor_tensor(
-                out=t[:],
-                in0=h_of[i][:],
-                scalar=neg_mean_of[i][:, 0:1],
-                in1=spread[:, 4 * v + g, :],
-                op0=ALU.add,
+        def normalise(u, n):
+            cols = slice(n * N_TILE, (n + 1) * N_TILE)
+            nc.vector.tensor_scalar(
+                out=z_of[u][:, cols],
+                in0=z_of[u][:, cols],
+                scalar1=mv_of[u][:, 0:1],
+                scalar2=rstd_of[u][:, 0:1],
+                op0=ALU.subtract,
                 op1=ALU.mult,
             )
-            t_of[i] = t
 
-        def scale_and_bias(i):
-            g, v, m = units[i]
-            nc.vector.scalar_tensor_tensor(
-                out=t_of[i][:],
-                in0=t_of[i][:],
-                scalar=rstd_of[i][:, 0:1],
-                in1=spread[:, 4 * v + 2 + g, :],
-                op0=ALU.mult,
-                op1=ALU.add,
+        def turn(u):
+            zt_of[u] = []
+            for n in range(N_TILES):
+                zt = psx.tile([P, J_BANK, P], F32, name="zt", tag="bank")
+                for jl in range(J_BANK):
+                    jt = J_BANK * n + jl
+                    nc.tensor.transpose(zt[:, jl, :], z_of[u][:, jt * P : (jt + 1) * P], ident_f[:])
+                zt_of[u].append(zt)
+
+        def gate(u, n):
+            g, v, m = units[u]
+            if n == 0:
+                gated = gpool.tile([P, J_TILES, P], F32, name="gated%d" % v)
+                gate_of[u] = gated
+            for jl in range(J_BANK):
+                jt = J_BANK * n + jl
+                col = 64 * v + 16 * g + jt
+                nc.scalar.activation(
+                    out=gate_of[u][:, jt, :],
+                    in_=zt_of[u][n][:, jl, :],
+                    func=(ACT.Sigmoid if v == 0 else ACT.Relu),
+                    scale=prm_t[:, col : col + 1],
+                    bias=prm_t[:, col + 32 : col + 33],
+                )
+
+        sum_of, back_of = {}, {}
+
+        def multiply(u, n):
+            blocks = slice(J_BANK * n, J_BANK * (n + 1))
+            nc.vector.tensor_tensor(
+                out=gate_of[u][:, blocks, :],
+                in0=gate_of[u][:, blocks, :],
+                in1=gate_of[u - MASKS][:, blocks, :],
+                op=ALU.mult,
             )
 
-        for step in range(n_units + 1):
-            if step < n_units:
-                g, v, m = units[step]
-                products(step)
-                if m == MASKS - 1 and step // MASKS + 2 < len(phases):
-                    loaded[phases[step // MASKS + 2]] = load_words(*phases[step // MASKS + 2])
-                if step == 0:
-                    quantise_group(1, transpose_group(1))
-                if step in (1, 2):
-                    rows = spread_matmuls(1, step - 1)
-                leave_psum(step)
-            k = step - 3
-            if k >= 0 and units[k][1] == 0:
-                nc.scalar.activation(out=t_of[k][:], in_=t_of[k][:], func=ACT.Sigmoid)
-            if step < n_units:
-                spread_of_row(step)
-                if step in (1, 2):
-                    spread_copies(rows, True)
-                centre_and_gain(step)
-            j = step - 1
-            if j >= 0:
-                g, v, m = units[j]
-                scale_and_bias(j)
-                if v == 1:
-                    nc.vector.scalar_tensor_tensor(
-                        out=t_of[j][:], in0=t_of[j][:], scalar=0.0, in1=t_of[j - MASKS][:], op0=ALU.max, op1=ALU.mult
-                    )
-                    if m == MASKS - 1:
-                        for n in range(N_TILES):
-                            cols = slice(n * N_TILE, (n + 1) * N_TILE)
-                            nc.vector.tensor_tensor(
-                                out=t_of[j - 1][:, cols], in0=t_of[j - 1][:, cols], in1=t_of[j][:, cols], op=ALU.add
-                            )
-                            nc.sync.dma_start(
-                                out=out[:, g * H + n * N_TILE : g * H + (n + 1) * N_TILE], in_=t_of[j - 1][:, cols]
-                            )
+        def add_masks(u, n):
+            g, v, m = units[u]
+            blocks = slice(J_BANK * n, J_BANK * (n + 1))
+            both = stage.tile([P, J_BANK, P], F32, name="both")
+            nc.vector.tensor_tensor(
+                out=both[:], in0=gate_of[u - 1][:, blocks, :], in1=gate_of[u][:, blocks, :], op=ALU.add
+            )
+            sum_of[(g, n)] = both
+
+        def turn_back(g, n):
+            back = psy.tile([P, J_BANK, P], F32, name="back", tag="bank")
+            for jl in range(J_BANK):
+                nc.tensor.transpose(back[:, jl, :], sum_of[(g, n)][:, jl, :], ident_f[:])
+            back_of[(g, n)] = back
+
+        def store(g, n):
+            result = stage.tile([P, N_TILE], F32, name="result")
+            nc.scalar.copy(out=result[:], in_=back_of[(g, n)][:].rearrange("p j b -> p (j b)"))
+            nc.sync.dma_start(out=out[:, g * H + n * N_TILE : g * H + (n + 1) * N_TILE], in_=result[:])
+
+        def weigh_run(jobs, sources):
+            previous = None
+            for g, c, m in jobs:
+                grouped = weigh(g, c, m, sources(c))
+                if previous is not None:
+                    quantise(*previous)
+                previous = (g, c, m, grouped)
+            quantise(*previous)
+
+        late = [(1, c, m) for c in range(PASSES) for m in range(MASKS)]
+        late_tiles = {}
+
+        def late_piece(i):
+            g, c, m = late[i]
+            late_tiles[i] = weigh(g, c, m, x1_words[:, c])
+            if i > 0:
+                quantise(*late[i - 1], late_tiles[i - 1])
+            if i == len(late) - 1:
+                quantise(*late[i], late_tiles[i])
+
+        for k in range(n_units + 2):
+            if k == 0:
+                weigh_run([(0, c, 0) for c in range(PASSES)], lambda c: x0_banks[c // 2][:, c % 2])
+                products(0, psx, False)
+                weigh_run([(0, c, 1) for c in range(PASSES)], lambda c: x0_banks[c // 2][:, c % 2])
+            elif k < n_units:
+                products(k, psy, True)
+            if k < n_units:
+                for n in range(N_TILES):
+                    leave_psum(k, n)
+            if k == 1:
+                loaded[(1, 1)] = load_words(1, 1)
+                x1_banks = transpose_group(1, psx)
+                for pair in range(PASSES // 2):
+                    nc.scalar.copy(out=x1_words[:, 2 * pair : 2 * pair + 2], in_=x1_banks[pair][:])
+            if 1 <= k <= n_units:
+                turn(k - 1)
+                for n in range(N_TILES):
+                    gate(k - 1, n)
+            if k == 6:
+                for n in range(N_TILES):
+                    turn_back(0, n)
+                for n in range(N_TILES):
+                    store(0, n)
+            for n in range(N_TILES):
+                if k < n_units:
+                    bank_stats(k, n)
+                if k in (2, 3):
+                    late_piece(N_TILES * (k - 2) + n)
+                if k >= 2 and units[k - 2][1] == 1:
+                    multiply(k - 2, n)
+                    if k - 2 == n_units - 1:
+                        add_masks(k - 2, n)
+                        turn_back(1, n)
+                        store(1, n)
+            if k < n_units:
+                row_stats(k)
+                for n in range(N_TILES):
+                    normalise(k, n)
+            if k == 5:
+                for n in range(N_TILES):
+                    add_masks(3, n)

@@ -29,8 +29,7 @@ ROWS = GROUPS * MASKS
 TAPS = PASSES * PACK
 ALPHA = 1.1
 EPS = 1e-5
-EXPONENT_COARSE = -29.0 / 32.0
-EXPONENT_REST = -1.0 / ALPHA - EXPONENT_COARSE
+CHUNKS = P // ROWS
 
 FLOPS = 2 * P * GROUPS * MASKS * S * H * 2
 
@@ -58,9 +57,8 @@ def tile_dynamicfeaturegroupinglayer_w_e_kernel(
         nc.vector.memset(planes[:].rearrange("p f n -> p (f n)").bitcast(I32), 0)
         ones = keep.tile([P, P], F32)
         nc.vector.memset(ones[:], 1.0)
-        exponents = keep.tile([P, 2, ROWS], F32)
-        nc.vector.memset(exponents[:, 0, :], EXPONENT_COARSE)
-        nc.vector.memset(exponents[:, 1, :], EXPONENT_REST)
+        exponent = keep.tile([P, ROWS], F32)
+        nc.vector.tensor_scalar_mul(out=exponent[:], in0=ones[:, 0:ROWS], scalar1=-1.0 / ALPHA)
         neg_half = keep.tile([P, 1], F32)
         nc.vector.memset(neg_half[:], -0.5)
         ident_f = keep.tile([P, P], F32)
@@ -68,13 +66,16 @@ def tile_dynamicfeaturegroupinglayer_w_e_kernel(
         ident_b = keep.tile([P, P], BF16)
         make_identity(nc, ident_b[:])
 
+        wc = keep.tile([P, S // CHUNKS], BF16)
+        nc.sync.dma_start(out=wc[:], in_=W_masks.rearrange("g m (i f) -> (g m i) f", i=CHUNKS))
         wm = keep.tile([P, ROWS, TAPS], BF16)
         nc.sync.dma_start(
             out=wm[:].rearrange("p a (c t) -> p (a c) t", t=PACK),
             in_=W_masks.rearrange("g m (c p t) -> p (g m c) t", c=PASSES, p=P, t=PACK),
         )
         x_sb = keep.tile([P, GROUPS * S], BF16)
-        nc.sync.dma_start(out=x_sb[:], in_=x)
+        for g in range(GROUPS):
+            nc.sync.dma_start(out=x_sb[:, g * S : (g + 1) * S], in_=x[:, g * S : (g + 1) * S])
         prm = keep.tile([P, P], BF16)
         for r in range(4):
             nc.scalar.dma_start(
@@ -146,39 +147,37 @@ def tile_dynamicfeaturegroupinglayer_w_e_kernel(
                 in_=grouped[:].rearrange("p b t -> p (b t)"),
             )
 
-        own_top = small.tile([P, ROWS], F32)
-        nc.vector.tensor_reduce(out=own_top[:], in_=wm[:], axis=AX.X, op=ALU.max)
-        tops = psx.tile([P, ROWS, P], F32, tag="bank")
-        for a in range(ROWS):
-            nc.tensor.transpose(tops[:, a, :], own_top[:, a : a + 1].to_broadcast([P, P]), ident_f[:])
+        piece_top = small.tile([P, 1], F32)
+        nc.vector.tensor_reduce(out=piece_top[:], in_=wc[:], axis=AX.X, op=ALU.max)
+        tops = psx.tile([P, ROWS, CHUNKS], F32, tag="bank")
+        nc.tensor.transpose(
+            tops[:].rearrange("p a i -> p (a i)"), piece_top[:, 0:1].to_broadcast([P, P]), ident_f[:]
+        )
         neg_top = small.tile([P, ROWS], F32)
         nc.vector.tensor_reduce(out=neg_top[:], in_=tops[:], axis=AX.X, op=ALU.max, negate=True)
-        neg_top_alpha = small.tile([P, ROWS], F32)
-        nc.vector.tensor_scalar_mul(out=neg_top_alpha[:], in0=neg_top[:], scalar1=ALPHA)
+        shifted = small.tile([P, ROWS, TAPS], F32)
+        nc.vector.tensor_tensor(
+            out=shifted[:], in0=wm[:], in1=neg_top[:].unsqueeze(2).to_broadcast([P, ROWS, TAPS]), op=ALU.add
+        )
         powered = small.tile([P, ROWS, TAPS], F32)
+        nc.scalar.activation(
+            out=powered[:].rearrange("p a t -> p (a t)"),
+            in_=shifted[:].rearrange("p a t -> p (a t)"),
+            func=ACT.Exp,
+            scale=ALPHA,
+        )
         part = small.tile([P, ROWS], F32)
-        for a in range(ROWS):
-            nc.scalar.activation(
-                out=powered[:, a, :],
-                in_=wm[:, a, :],
-                func=ACT.Exp,
-                scale=ALPHA,
-                bias=neg_top_alpha[:, a : a + 1],
-                accum_out=part[:, a : a + 1],
-            )
+        nc.vector.tensor_reduce(out=part[:], in_=powered[:], axis=AX.X, op=ALU.add)
         total_ps = psx.tile([P, ROWS], F32, tag="bank")
         nc.tensor.matmul(out=total_ps[:], lhsT=ones[:], rhs=part[:], start=True, stop=True)
         e = small.tile([P, ROWS, TAPS], F32)
-        for a in range(ROWS):
-            nc.scalar.activation(out=e[:, a, :], in_=wm[:, a, :], func=ACT.Exp, bias=neg_top[:, a : a + 1])
+        nc.scalar.activation(
+            out=e[:].rearrange("p a t -> p (a t)"), in_=shifted[:].rearrange("p a t -> p (a t)"), func=ACT.Exp
+        )
         total = small.tile([P, ROWS], F32)
         nc.vector.tensor_scalar_add(out=total[:], in0=total_ps[:], scalar1=EPS)
-        factors = small.tile([P, 2, ROWS], F32)
-        nc.gpsimd.tensor_tensor(
-            out=factors[:], in0=total[:].unsqueeze(1).to_broadcast([P, 2, ROWS]), in1=exponents[:], op=ALU.pow
-        )
         inv_norm = small.tile([P, ROWS], F32)
-        nc.vector.tensor_tensor(out=inv_norm[:], in0=factors[:, 0, :], in1=factors[:, 1, :], op=ALU.mult)
+        nc.gpsimd.tensor_tensor(out=inv_norm[:], in0=total[:], in1=exponent[:], op=ALU.pow)
         nc.vector.tensor_tensor(
             out=mask[:], in0=e[:], in1=inv_norm[:].unsqueeze(2).to_broadcast([P, ROWS, TAPS]), op=ALU.mult
         )
@@ -193,7 +192,7 @@ def tile_dynamicfeaturegroupinglayer_w_e_kernel(
 
         units = [(g, v, m) for g in range(GROUPS) for v in range(2) for m in range(MASKS)]
         n_units = len(units)
-        banks_of, mv_of, rstd_of, z_of, zt_of, gate_of, stats_of = {}, {}, {}, {}, {}, {}, {}
+        banks_of, nbias_of, rstd_of, z_of, zt_of, gate_of, stats_of = {}, {}, {}, {}, {}, {}, {}
 
         def one_pass(u, c, n):
             g, v, m = units[u]
@@ -244,17 +243,21 @@ def tile_dynamicfeaturegroupinglayer_w_e_kernel(
             nc.vector.tensor_scalar_add(out=var_eps[:], in0=mv[:, 1:2], scalar1=EPS)
             rstd = small.tile([P, 1], F32, name="rstd")
             nc.gpsimd.tensor_tensor(out=rstd[:], in0=var_eps[:], in1=neg_half[:], op=ALU.pow)
-            mv_of[u], rstd_of[u] = mv, rstd
+            nbias = small.tile([P, 1], F32, name="nbias")
+            nc.gpsimd.tensor_scalar(
+                out=nbias[:], in0=mv[:, 0:1], scalar1=rstd[:, 0:1], scalar2=-1.0, op0=ALU.mult, op1=ALU.mult
+            )
+            nbias_of[u], rstd_of[u] = nbias, rstd
 
-        def normalise(u, n):
+        def normalise(u, n, engine):
             cols = slice(n * N_TILE, (n + 1) * N_TILE)
-            nc.vector.tensor_scalar(
+            engine.tensor_scalar(
                 out=z_of[u][:, cols],
                 in0=z_of[u][:, cols],
-                scalar1=mv_of[u][:, 0:1],
-                scalar2=rstd_of[u][:, 0:1],
-                op0=ALU.subtract,
-                op1=ALU.mult,
+                scalar1=rstd_of[u][:, 0:1],
+                scalar2=nbias_of[u][:, 0:1],
+                op0=ALU.mult,
+                op1=ALU.add,
             )
 
         def turn(u):
@@ -363,15 +366,26 @@ def tile_dynamicfeaturegroupinglayer_w_e_kernel(
                 if k in (2, 3):
                     late_piece(N_TILES * (k - 2) + n)
                 if k >= 2 and units[k - 2][1] == 1:
-                    multiply(k - 2, n)
+                    if k - 2 != n_units - 2:
+                        multiply(k - 2, n)
                     if k - 2 == n_units - 1:
                         add_masks(k - 2, n)
                         turn_back(1, n)
                         store(1, n)
-            if k < n_units:
+            if k < n_units - 1:
                 row_stats(k)
                 for n in range(N_TILES):
-                    normalise(k, n)
+                    normalise(k, n, nc.gpsimd)
+            if k == n_units - 1:
+                row_stats(k)
+                multiply(k - 1, 0)
+                multiply(k - 1, 1)
+                normalise(k, 0, nc.gpsimd)
+                normalise(k, 1, nc.gpsimd)
+                normalise(k, 2, nc.vector)
+                normalise(k, 3, nc.vector)
+                multiply(k - 1, 2)
+                multiply(k - 1, 3)
             if k == 5:
                 for n in range(N_TILES):
                     add_masks(3, n)

@@ -111,40 +111,37 @@ def tile_dynamicfeaturegroupinglayer_w_e_kernel(
 
         a_codes = keep.tile([P, GROUPS * PASSES, MASKS * P], U32, align_bytes=64)
         a_scales = keep.tile([P, GROUPS * PASSES, MASKS * P], U8, align_bytes=64)
-        x_words = x_sb[:].bitcast(F32)
+        x_pairs = x_sb[:].bitcast(F32)
         mask = keep.tile([P, ROWS, TAPS], F32)
+        x_words = keep.tile([P, GROUPS * PASSES, 2, P], F32)
 
-        def transpose_group(g, pool):
-            banks = []
-            for pair in range(PASSES // 2):
-                xt = pool.tile([P, 2, 2, P], F32, name="xt", tag="bank")
-                for i in range(2):
-                    gp = PASSES * g + 2 * pair + i
-                    for u in range(2):
-                        nc.tensor.transpose(
-                            xt[:, i, u, :], x_words[:, 256 * gp + u : 256 * (gp + 1) : 2], ident_f[:]
-                        )
-                banks.append(xt)
-            return banks
+        def turn_x(pair):
+            xt = psy.tile([P, 2, 2, P], F32, name="xt", tag="bank")
+            for i in range(2):
+                gp = 2 * pair + i
+                for u in range(2):
+                    nc.tensor.transpose(xt[:, i, u, :], x_pairs[:, 256 * gp + u : 256 * (gp + 1) : 2], ident_f[:])
+            return xt
 
-        def weigh(g, c, m, words):
-            grouped = stage.tile([P, P, PACK], BF16, name="grouped", align_bytes=64)
-            nc.vector.tensor_tensor(
-                out=grouped[:].rearrange("p b (u e) -> p b u e", e=2),
-                in0=words.bitcast(BF16).rearrange("p u (b e) -> p b u e", e=2),
-                in1=mask[:, MASKS * g + m, PACK * c : PACK * (c + 1)]
-                .rearrange("p (u e) -> p u e", e=2)
-                .unsqueeze(1)
-                .to_broadcast([P, P, 2, 2]),
-                op=ALU.mult,
-            )
+        def weigh(gp):
+            grouped = stage.tile([P, MASKS, P, PACK], BF16, name="grouped", align_bytes=64)
+            for m in range(MASKS):
+                nc.vector.tensor_tensor(
+                    out=grouped[:, m].rearrange("p b (u e) -> p b u e", e=2),
+                    in0=x_words[:, gp].bitcast(BF16).rearrange("p u (b e) -> p b u e", e=2),
+                    in1=mask[:, MASKS * (gp // PASSES) + m, PACK * (gp % PASSES) : PACK * (gp % PASSES + 1)]
+                    .rearrange("p (u e) -> p u e", e=2)
+                    .unsqueeze(1)
+                    .to_broadcast([P, P, 2, 2]),
+                    op=ALU.mult,
+                )
             return grouped
 
-        def quantise(g, c, m, grouped):
+        def quantise(gp, grouped):
             nc.vector.quantize_mx(
-                out=a_codes[:, PASSES * g + c, m * P : (m + 1) * P].bitcast(FP8X4),
-                scales=a_scales[:, PASSES * g + c, m * P : (m + 1) * P],
-                in_=grouped[:].rearrange("p b t -> p (b t)"),
+                out=a_codes[:, gp, :].bitcast(FP8X4),
+                scales=a_scales[:, gp, :],
+                in_=grouped[:].rearrange("p m b t -> p (m b t)"),
             )
 
         piece_top = small.tile([P, 1], F32)
@@ -168,6 +165,7 @@ def tile_dynamicfeaturegroupinglayer_w_e_kernel(
         )
         part = small.tile([P, ROWS], F32)
         nc.vector.tensor_reduce(out=part[:], in_=powered[:], axis=AX.X, op=ALU.add)
+        x_banks = [turn_x(0)]
         total_ps = psx.tile([P, ROWS], F32, tag="bank")
         nc.tensor.matmul(out=total_ps[:], lhsT=ones[:], rhs=part[:], start=True, stop=True)
         e = small.tile([P, ROWS, TAPS], F32)
@@ -181,18 +179,29 @@ def tile_dynamicfeaturegroupinglayer_w_e_kernel(
         nc.vector.tensor_tensor(
             out=mask[:], in0=e[:], in1=inv_norm[:].unsqueeze(2).to_broadcast([P, ROWS, TAPS]), op=ALU.mult
         )
-        x0_banks = transpose_group(0, psy)
+        for pair in range(1, GROUPS * PASSES // 2):
+            x_banks.append(turn_x(pair))
         prm_ps = psx.tile([P, P], BF16, tag="bank")
         nc.tensor.transpose(prm_ps[:], prm[:], ident_b[:])
         warm = small.tile([P, 1], F32)
-        nc.scalar.activation(out=warm[:], in_=neg_half[:], func=ACT.Sigmoid)
+        for pair in range(GROUPS * PASSES // 2):
+            nc.scalar.copy(out=x_words[:, 2 * pair : 2 * pair + 2], in_=x_banks[pair][:])
+            if pair == 1:
+                nc.scalar.activation(out=warm[:], in_=neg_half[:], func=ACT.Sigmoid)
         prm_t = keep.tile([P, P], F32)
         nc.scalar.copy(out=prm_t[:], in_=prm_ps[:])
-        x1_words = keep.tile([P, PASSES, 2, P], F32)
 
         units = [(g, v, m) for g in range(GROUPS) for v in range(2) for m in range(MASKS)]
         n_units = len(units)
-        banks_of, nbias_of, rstd_of, z_of, zt_of, gate_of, stats_of = {}, {}, {}, {}, {}, {}, {}
+        banks_of, mv_of, rstd_of, z_of, zt_of, gate_of, stats_of = {}, {}, {}, {}, {}, {}, {}
+        sum_of, back_of = {}, {}
+        ORDER = (0, 1, 2, 3)
+
+        def open_banks(u, pool):
+            banks_of[u] = []
+            for n in range(N_TILES):
+                acc = pool.tile([P, N_TILE], F32, name="acc", tag="bank")
+                banks_of[u].append(acc)
 
         def one_pass(u, c, n):
             g, v, m = units[u]
@@ -208,33 +217,40 @@ def tile_dynamicfeaturegroupinglayer_w_e_kernel(
                 stop=(c == PASSES - 1),
             )
 
-        def products(u, pool, bank_by_bank):
-            banks_of[u] = []
-            if bank_by_bank:
-                for n in range(N_TILES):
-                    acc = pool.tile([P, N_TILE], F32, name="acc", tag="bank")
-                    banks_of[u].append(acc)
-                    for c in range(PASSES):
-                        one_pass(u, c, n)
-            else:
-                for n in range(N_TILES):
-                    acc = pool.tile([P, N_TILE], F32, name="acc", tag="bank")
-                    banks_of[u].append(acc)
-                for c in range(PASSES):
-                    for n in range(N_TILES):
-                        one_pass(u, c, n)
+        def chunk_passes(u, c):
+            for n in range(N_TILES):
+                one_pass(u, c, n)
 
-        def leave_psum(u, n):
-            if n == 0:
-                z = zpool.tile([P, H], F32, name="z")
-                z_of[u] = z
-            nc.scalar.copy(out=z_of[u][:, n * N_TILE : (n + 1) * N_TILE], in_=banks_of[u][n][:])
+        def bank_by_bank(u):
+            banks_of[u] = []
+            for n in range(N_TILES):
+                acc = psx.tile([P, N_TILE], F32, name="acc", tag="bank")
+                banks_of[u].append(acc)
+                for c in range(PASSES):
+                    one_pass(u, c, n)
+
+        def leave_psum(u):
+            z = zpool.tile([P, H], F32, name="z")
+            z_of[u] = z
+            for n in range(N_TILES):
+                nc.scalar.copy(out=z[:, n * N_TILE : (n + 1) * N_TILE], in_=banks_of[u][n][:])
 
         def bank_stats(u, n):
             if n == 0:
                 stats = small.tile([P, N_TILES, 6], F32, name="stats")
                 stats_of[u] = stats
             nc.vector.bn_stats(out=stats_of[u][:, n, :], in_=z_of[u][:, n * N_TILE : (n + 1) * N_TILE])
+
+        def normalise(u, n):
+            cols = slice(n * N_TILE, (n + 1) * N_TILE)
+            nc.vector.tensor_scalar(
+                out=z_of[u][:, cols],
+                in0=z_of[u][:, cols],
+                scalar1=mv_of[u][:, 0:1],
+                scalar2=rstd_of[u][:, 0:1],
+                op0=ALU.subtract,
+                op1=ALU.mult,
+            )
 
         def row_stats(u):
             mv = small.tile([P, 2], F32, name="mv")
@@ -243,35 +259,22 @@ def tile_dynamicfeaturegroupinglayer_w_e_kernel(
             nc.vector.tensor_scalar_add(out=var_eps[:], in0=mv[:, 1:2], scalar1=EPS)
             rstd = small.tile([P, 1], F32, name="rstd")
             nc.gpsimd.tensor_tensor(out=rstd[:], in0=var_eps[:], in1=neg_half[:], op=ALU.pow)
-            nbias = small.tile([P, 1], F32, name="nbias")
-            nc.gpsimd.tensor_scalar(
-                out=nbias[:], in0=mv[:, 0:1], scalar1=rstd[:, 0:1], scalar2=-1.0, op0=ALU.mult, op1=ALU.mult
-            )
-            nbias_of[u], rstd_of[u] = nbias, rstd
+            mv_of[u], rstd_of[u] = mv, rstd
 
-        def normalise(u, n, engine):
-            cols = slice(n * N_TILE, (n + 1) * N_TILE)
-            engine.tensor_scalar(
-                out=z_of[u][:, cols],
-                in0=z_of[u][:, cols],
-                scalar1=rstd_of[u][:, 0:1],
-                scalar2=nbias_of[u][:, 0:1],
-                op0=ALU.mult,
-                op1=ALU.add,
-            )
-
-        def turn(u):
-            zt_of[u] = []
+        def finish_rows(u):
             for n in range(N_TILES):
-                zt = psx.tile([P, J_BANK, P], F32, name="zt", tag="bank")
-                for jl in range(J_BANK):
-                    jt = J_BANK * n + jl
-                    nc.tensor.transpose(zt[:, jl, :], z_of[u][:, jt * P : (jt + 1) * P], ident_f[:])
-                zt_of[u].append(zt)
+                normalise(u, n)
+
+        def turn(u, n):
+            zt = psy.tile([P, J_BANK, P], F32, name="zt", tag="bank")
+            for jl in range(J_BANK):
+                jt = J_BANK * n + jl
+                nc.tensor.transpose(zt[:, jl, :], z_of[u][:, jt * P : (jt + 1) * P], ident_f[:])
+            zt_of[(u, n)] = zt
 
         def gate(u, n):
             g, v, m = units[u]
-            if n == 0:
+            if u not in gate_of:
                 gated = gpool.tile([P, J_TILES, P], F32, name="gated%d" % v)
                 gate_of[u] = gated
             for jl in range(J_BANK):
@@ -279,13 +282,17 @@ def tile_dynamicfeaturegroupinglayer_w_e_kernel(
                 col = 64 * v + 16 * g + jt
                 nc.scalar.activation(
                     out=gate_of[u][:, jt, :],
-                    in_=zt_of[u][n][:, jl, :],
+                    in_=zt_of[(u, n)][:, jl, :],
                     func=(ACT.Sigmoid if v == 0 else ACT.Relu),
                     scale=prm_t[:, col : col + 1],
                     bias=prm_t[:, col + 32 : col + 33],
                 )
 
-        sum_of, back_of = {}, {}
+        def turn_and_gate(u, some):
+            for n in some:
+                turn(u, n)
+            for n in some:
+                gate(u, n)
 
         def multiply(u, n):
             blocks = slice(J_BANK * n, J_BANK * (n + 1))
@@ -306,86 +313,120 @@ def tile_dynamicfeaturegroupinglayer_w_e_kernel(
             sum_of[(g, n)] = both
 
         def turn_back(g, n):
-            back = psy.tile([P, J_BANK, P], F32, name="back", tag="bank")
+            back = psx.tile([P, J_BANK, P], F32, name="back", tag="bank")
             for jl in range(J_BANK):
                 nc.tensor.transpose(back[:, jl, :], sum_of[(g, n)][:, jl, :], ident_f[:])
             back_of[(g, n)] = back
 
-        def store(g, n):
+        def store(g, n, by_vector):
             result = stage.tile([P, N_TILE], F32, name="result")
-            nc.scalar.copy(out=result[:], in_=back_of[(g, n)][:].rearrange("p j b -> p (j b)"))
+            if by_vector:
+                nc.vector.tensor_copy(out=result[:], in_=back_of[(g, n)][:].rearrange("p j b -> p (j b)"))
+            else:
+                nc.scalar.copy(out=result[:], in_=back_of[(g, n)][:].rearrange("p j b -> p (j b)"))
             nc.sync.dma_start(out=out[:, g * H + n * N_TILE : g * H + (n + 1) * N_TILE], in_=result[:])
 
-        def weigh_run(jobs, sources):
-            previous = None
-            for g, c, m in jobs:
-                grouped = weigh(g, c, m, sources(c))
-                if previous is not None:
-                    quantise(*previous)
-                previous = (g, c, m, grouped)
-            quantise(*previous)
+        previous = None
+        for gp in range(GROUPS * PASSES):
+            grouped = weigh(gp)
+            if previous is not None:
+                quantise(gp - 1, previous)
+            previous = grouped
+        quantise(GROUPS * PASSES - 1, previous)
 
-        late = [(1, c, m) for c in range(PASSES) for m in range(MASKS)]
-        late_tiles = {}
+        open_banks(0, psx)
+        open_banks(1, psy)
+        for c in range(PASSES):
+            chunk_passes(0, c)
+            chunk_passes(1, c)
+        loaded[(1, 1)] = load_words(1, 1)
+        leave_psum(0)
+        leave_psum(1)
+        for n in range(N_TILES):
+            bank_stats(0, n)
+        row_stats(0)
+        bank_stats(1, 0)
+        bank_stats(1, 1)
+        finish_rows(0)
+        bank_stats(1, 2)
+        bank_stats(1, 3)
+        row_stats(1)
+        finish_rows(1)
 
-        def late_piece(i):
-            g, c, m = late[i]
-            late_tiles[i] = weigh(g, c, m, x1_words[:, c])
-            if i > 0:
-                quantise(*late[i - 1], late_tiles[i - 1])
-            if i == len(late) - 1:
-                quantise(*late[i], late_tiles[i])
+        open_banks(2, psx)
+        chunk_passes(2, 0)
+        chunk_passes(2, 1)
+        turn_and_gate(0, ORDER[:2])
+        chunk_passes(2, 2)
+        turn_and_gate(0, ORDER[2:])
+        chunk_passes(2, 3)
+        leave_psum(2)
+        turn_and_gate(1, ORDER)
+        for n in range(N_TILES):
+            bank_stats(2, n)
+        row_stats(2)
+        finish_rows(2)
 
-        for k in range(n_units + 2):
-            if k == 0:
-                weigh_run([(0, c, 0) for c in range(PASSES)], lambda c: x0_banks[c // 2][:, c % 2])
-                products(0, psx, False)
-                weigh_run([(0, c, 1) for c in range(PASSES)], lambda c: x0_banks[c // 2][:, c % 2])
-            elif k < n_units:
-                products(k, psy, True)
-            if k < n_units:
-                for n in range(N_TILES):
-                    leave_psum(k, n)
-            if k == 1:
-                loaded[(1, 1)] = load_words(1, 1)
-                x1_banks = transpose_group(1, psx)
-                for pair in range(PASSES // 2):
-                    nc.scalar.copy(out=x1_words[:, 2 * pair : 2 * pair + 2], in_=x1_banks[pair][:])
-            if 1 <= k <= n_units:
-                turn(k - 1)
-                for n in range(N_TILES):
-                    gate(k - 1, n)
-            if k == 6:
-                for n in range(N_TILES):
-                    turn_back(0, n)
-                for n in range(N_TILES):
-                    store(0, n)
-            for n in range(N_TILES):
-                if k < n_units:
-                    bank_stats(k, n)
-                if k in (2, 3):
-                    late_piece(N_TILES * (k - 2) + n)
-                if k >= 2 and units[k - 2][1] == 1:
-                    if k - 2 != n_units - 2:
-                        multiply(k - 2, n)
-                    if k - 2 == n_units - 1:
-                        add_masks(k - 2, n)
-                        turn_back(1, n)
-                        store(1, n)
-            if k < n_units - 1:
-                row_stats(k)
-                for n in range(N_TILES):
-                    normalise(k, n, nc.gpsimd)
-            if k == n_units - 1:
-                row_stats(k)
-                multiply(k - 1, 0)
-                multiply(k - 1, 1)
-                normalise(k, 0, nc.gpsimd)
-                normalise(k, 1, nc.gpsimd)
-                normalise(k, 2, nc.vector)
-                normalise(k, 3, nc.vector)
-                multiply(k - 1, 2)
-                multiply(k - 1, 3)
-            if k == 5:
-                for n in range(N_TILES):
-                    add_masks(3, n)
+        def chunk_by_chunk(u):
+            open_banks(u, psx)
+            for c in range(PASSES):
+                chunk_passes(u, c)
+
+        bank_by_bank(3)
+        leave_psum(3)
+        turn_and_gate(2, ORDER)
+        for n in range(N_TILES):
+            bank_stats(3, n)
+        row_stats(3)
+        finish_rows(3)
+
+        chunk_by_chunk(4)
+        leave_psum(4)
+        turn_and_gate(3, ORDER)
+        for n in ORDER:
+            multiply(2, n)
+        for n in range(N_TILES):
+            bank_stats(4, n)
+        row_stats(4)
+        finish_rows(4)
+
+        bank_by_bank(5)
+        leave_psum(5)
+        turn_and_gate(4, ORDER)
+        for n in range(N_TILES):
+            bank_stats(5, n)
+            multiply(3, ORDER[n])
+        row_stats(5)
+        add_masks(3, 0)
+        finish_rows(5)
+        for n in range(1, N_TILES):
+            add_masks(3, n)
+
+        chunk_by_chunk(6)
+        leave_psum(6)
+        bank_by_bank(7)
+        leave_psum(7)
+        for n in range(N_TILES):
+            bank_stats(6, n)
+        row_stats(6)
+        finish_rows(6)
+        turn_and_gate(5, ORDER)
+        for n in range(N_TILES):
+            turn_back(0, n)
+        for n in range(N_TILES):
+            bank_stats(7, n)
+        row_stats(7)
+        store(0, 0, True)
+        store(0, 1, True)
+        finish_rows(7)
+        store(0, 2, True)
+        store(0, 3, True)
+        turn_and_gate(6, ORDER)
+        for n in ORDER:
+            multiply(6, n)
+        turn_and_gate(7, ORDER)
+        for n in ORDER:
+            multiply(7, n)
+            add_masks(7, n)
+            turn_back(1, n)
+            store(1, n, False)

@@ -194,7 +194,7 @@ def tile_dynamicfeaturegroupinglayer_w_e_kernel(
         units = [(g, v, m) for g in range(GROUPS) for v in range(2) for m in range(MASKS)]
         n_units = len(units)
         banks_of, mv_of, rstd_of, z_of, zt_of, gate_of, stats_of = {}, {}, {}, {}, {}, {}, {}
-        sum_of, back_of = {}, {}
+        back_of = {}
         ORDER = (0, 1, 2, 3)
 
         def open_banks(u, pool):
@@ -303,19 +303,19 @@ def tile_dynamicfeaturegroupinglayer_w_e_kernel(
                 op=ALU.mult,
             )
 
-        def add_masks(u, n):
-            g, v, m = units[u]
-            blocks = slice(J_BANK * n, J_BANK * (n + 1))
-            both = stage.tile([P, J_BANK, P], F32, name="both")
-            nc.vector.tensor_tensor(
-                out=both[:], in0=gate_of[u - 1][:, blocks, :], in1=gate_of[u][:, blocks, :], op=ALU.add
-            )
-            sum_of[(g, n)] = both
-
         def turn_back(g, n):
             back = psx.tile([P, J_BANK, P], F32, name="back", tag="bank")
+            first = 2 * MASKS * g + MASKS
             for jl in range(J_BANK):
-                nc.tensor.transpose(back[:, jl, :], sum_of[(g, n)][:, jl, :], ident_f[:])
+                for m in range(MASKS):
+                    nc.tensor.matmul(
+                        out=back[:, jl, :],
+                        lhsT=gate_of[first + m][:, J_BANK * n + jl, :],
+                        rhs=ident_f[:],
+                        is_transpose=True,
+                        start=(m == 0),
+                        stop=(m == MASKS - 1),
+                    )
             back_of[(g, n)] = back
 
         def store(g, n, by_vector):
@@ -397,10 +397,7 @@ def tile_dynamicfeaturegroupinglayer_w_e_kernel(
             bank_stats(5, n)
             multiply(3, ORDER[n])
         row_stats(5)
-        add_masks(3, 0)
         finish_rows(5)
-        for n in range(1, N_TILES):
-            add_masks(3, n)
 
         chunk_by_chunk(6)
         leave_psum(6)
@@ -427,6 +424,5 @@ def tile_dynamicfeaturegroupinglayer_w_e_kernel(
         turn_and_gate(7, ORDER)
         for n in ORDER:
             multiply(7, n)
-            add_masks(7, n)
             turn_back(1, n)
             store(1, n, False)

@@ -47,9 +47,10 @@ def tile_dynamicfeaturegroupinglayer_w_e_kernel(
         keep = ctx.enter_context(tc.tile_pool(name="keep", bufs=1))
         small = ctx.enter_context(tc.tile_pool(name="small", bufs=4))
         stage = ctx.enter_context(tc.tile_pool(name="stage", bufs=4))
-        wpool = ctx.enter_context(tc.tile_pool(name="wpool", bufs=12))
-        zpool = ctx.enter_context(tc.tile_pool(name="zpool", bufs=3))
-        gpool = ctx.enter_context(tc.tile_pool(name="gpool", bufs=2))
+        wpool = ctx.enter_context(tc.tile_pool(name="wpool", bufs=10))
+        zpool = ctx.enter_context(tc.tile_pool(name="zpool", bufs=4))
+        spool = ctx.enter_context(tc.tile_pool(name="spool", bufs=2))
+        rpool = ctx.enter_context(tc.tile_pool(name="rpool", bufs=4))
         psx = ctx.enter_context(tc.psum_pool(name="psx", bufs=4))
         psy = ctx.enter_context(tc.psum_pool(name="psy", bufs=4))
 
@@ -100,14 +101,27 @@ def tile_dynamicfeaturegroupinglayer_w_e_kernel(
                 chunks.append(chunk)
             return chunks
 
-        phases = [(g, v) for g in range(GROUPS) for v in range(2)]
+        def load_columns(g, v):
+            tiles = []
+            for n in range(N_TILES):
+                chunk = wpool.tile([P, PASSES, N_TILE], U32, name="chunk", align_bytes=64)
+                nc.sync.dma_start(
+                    out=chunk[:].bitcast(I32),
+                    in_=w_words[v][PASSES * g : PASSES * (g + 1), :, n * N_TILE : (n + 1) * N_TILE, :]
+                    .rearrange("c p n t -> p c (n t)")
+                    .bitcast(I32),
+                )
+                tiles.append(chunk)
+            return tiles
+
         loaded = {}
         load_scales(0, 0)
         loaded[(0, 0)] = load_words(0, 0)
-        for g, v in phases[1:]:
-            load_scales(g, v)
-        loaded[(0, 1)] = load_words(0, 1)
-        loaded[(1, 0)] = load_words(1, 0)
+        load_scales(0, 1)
+        loaded[(0, 1)] = load_columns(0, 1)
+        load_scales(1, 0)
+        load_scales(1, 1)
+        loaded[(1, 0)] = load_columns(1, 0)
 
         a_codes = keep.tile([P, GROUPS * PASSES, MASKS * P], U32, align_bytes=64)
         a_scales = keep.tile([P, GROUPS * PASSES, MASKS * P], U8, align_bytes=64)
@@ -123,7 +137,7 @@ def tile_dynamicfeaturegroupinglayer_w_e_kernel(
                     nc.tensor.transpose(xt[:, i, u, :], x_pairs[:, 256 * gp + u : 256 * (gp + 1) : 2], ident_f[:])
             return xt
 
-        def weigh(gp):
+        def weigh(gp, at_once):
             grouped = stage.tile([P, MASKS, P, PACK], BF16, name="grouped", align_bytes=64)
             for m in range(MASKS):
                 nc.vector.tensor_tensor(
@@ -135,6 +149,12 @@ def tile_dynamicfeaturegroupinglayer_w_e_kernel(
                     .to_broadcast([P, P, 2, 2]),
                     op=ALU.mult,
                 )
+                if at_once:
+                    nc.vector.quantize_mx(
+                        out=a_codes[:, gp, m * P : (m + 1) * P].bitcast(FP8X4),
+                        scales=a_scales[:, gp, m * P : (m + 1) * P],
+                        in_=grouped[:, m].rearrange("p b t -> p (b t)"),
+                    )
             return grouped
 
         def quantise(gp, grouped):
@@ -211,7 +231,7 @@ def tile_dynamicfeaturegroupinglayer_w_e_kernel(
                 out=banks_of[u][n][:],
                 lhsT=a_codes[:, gp, m * P : (m + 1) * P].bitcast(FP8X4),
                 lhsT_scale=a_scales[:, gp, m * P : (m + 1) * P],
-                rhs=loaded[(g, v)][c][:, cols].bitcast(FP8X4),
+                rhs=(loaded[(g, v)][c][:, cols] if (g, v) == (0, 0) else loaded[(g, v)][n][:, c, :]).bitcast(FP8X4),
                 rhs_scale=planes[4 * c : P, 2 * g + v, cols],
                 start=(c == 0),
                 stop=(c == PASSES - 1),
@@ -221,19 +241,25 @@ def tile_dynamicfeaturegroupinglayer_w_e_kernel(
             for n in range(N_TILES):
                 one_pass(u, c, n)
 
+        def one_bank(u, n):
+            acc = psx.tile([P, N_TILE], F32, name="acc", tag="bank")
+            banks_of.setdefault(u, []).append(acc)
+            for c in range(PASSES):
+                one_pass(u, c, n)
+
         def bank_by_bank(u):
-            banks_of[u] = []
             for n in range(N_TILES):
-                acc = psx.tile([P, N_TILE], F32, name="acc", tag="bank")
-                banks_of[u].append(acc)
-                for c in range(PASSES):
-                    one_pass(u, c, n)
+                one_bank(u, n)
+
+        def leave_bank(u, n):
+            if n == 0:
+                z = zpool.tile([P, H], F32, name="z")
+                z_of[u] = z
+            nc.scalar.copy(out=z_of[u][:, n * N_TILE : (n + 1) * N_TILE], in_=banks_of[u][n][:])
 
         def leave_psum(u):
-            z = zpool.tile([P, H], F32, name="z")
-            z_of[u] = z
             for n in range(N_TILES):
-                nc.scalar.copy(out=z[:, n * N_TILE : (n + 1) * N_TILE], in_=banks_of[u][n][:])
+                leave_bank(u, n)
 
         def bank_stats(u, n):
             if n == 0:
@@ -241,8 +267,8 @@ def tile_dynamicfeaturegroupinglayer_w_e_kernel(
                 stats_of[u] = stats
             nc.vector.bn_stats(out=stats_of[u][:, n, :], in_=z_of[u][:, n * N_TILE : (n + 1) * N_TILE])
 
-        def normalise(u, n):
-            cols = slice(n * N_TILE, (n + 1) * N_TILE)
+        def normalise(u, first, banks):
+            cols = slice(first * N_TILE, (first + banks) * N_TILE)
             nc.vector.tensor_scalar(
                 out=z_of[u][:, cols],
                 in0=z_of[u][:, cols],
@@ -256,14 +282,16 @@ def tile_dynamicfeaturegroupinglayer_w_e_kernel(
             mv = small.tile([P, 2], F32, name="mv")
             nc.vector.bn_aggr(out=mv[:], in_=stats_of[u][:].rearrange("p n s -> p (n s)"))
             var_eps = small.tile([P, 1], F32, name="var_eps")
-            nc.vector.tensor_scalar_add(out=var_eps[:], in0=mv[:, 1:2], scalar1=EPS)
+            nc.gpsimd.tensor_scalar(
+                out=var_eps[:], in0=mv[:, 1:2], scalar1=1.0, scalar2=EPS, op0=ALU.mult, op1=ALU.add
+            )
             rstd = small.tile([P, 1], F32, name="rstd")
             nc.gpsimd.tensor_tensor(out=rstd[:], in0=var_eps[:], in1=neg_half[:], op=ALU.pow)
             mv_of[u], rstd_of[u] = mv, rstd
 
-        def finish_rows(u):
-            for n in range(N_TILES):
-                normalise(u, n)
+        def finish_rows(u, pieces):
+            for i in range(pieces):
+                normalise(u, i * N_TILES // pieces, N_TILES // pieces)
 
         def turn(u, n):
             zt = psy.tile([P, J_BANK, P], F32, name="zt", tag="bank")
@@ -275,7 +303,7 @@ def tile_dynamicfeaturegroupinglayer_w_e_kernel(
         def gate(u, n):
             g, v, m = units[u]
             if u not in gate_of:
-                gated = gpool.tile([P, J_TILES, P], F32, name="gated%d" % v)
+                gated = (spool if v == 0 else rpool).tile([P, J_TILES, P], F32, name="gated")
                 gate_of[u] = gated
             for jl in range(J_BANK):
                 jt = J_BANK * n + jl
@@ -294,8 +322,8 @@ def tile_dynamicfeaturegroupinglayer_w_e_kernel(
             for n in some:
                 gate(u, n)
 
-        def multiply(u, n):
-            blocks = slice(J_BANK * n, J_BANK * (n + 1))
+        def multiply(u, n, banks=1):
+            blocks = slice(J_BANK * n, J_BANK * (n + banks))
             nc.vector.tensor_tensor(
                 out=gate_of[u][:, blocks, :],
                 in0=gate_of[u][:, blocks, :],
@@ -326,9 +354,10 @@ def tile_dynamicfeaturegroupinglayer_w_e_kernel(
                 nc.scalar.copy(out=result[:], in_=back_of[(g, n)][:].rearrange("p j b -> p (j b)"))
             nc.sync.dma_start(out=out[:, g * H + n * N_TILE : g * H + (n + 1) * N_TILE], in_=result[:])
 
+        weigh(0, True)
         previous = None
-        for gp in range(GROUPS * PASSES):
-            grouped = weigh(gp)
+        for gp in range(1, GROUPS * PASSES):
+            grouped = weigh(gp, False)
             if previous is not None:
                 quantise(gp - 1, previous)
             previous = grouped
@@ -339,7 +368,7 @@ def tile_dynamicfeaturegroupinglayer_w_e_kernel(
         for c in range(PASSES):
             chunk_passes(0, c)
             chunk_passes(1, c)
-        loaded[(1, 1)] = load_words(1, 1)
+        loaded[(1, 1)] = load_columns(1, 1)
         leave_psum(0)
         leave_psum(1)
         for n in range(N_TILES):
@@ -347,81 +376,64 @@ def tile_dynamicfeaturegroupinglayer_w_e_kernel(
         row_stats(0)
         bank_stats(1, 0)
         bank_stats(1, 1)
-        finish_rows(0)
+        finish_rows(0, 1)
         bank_stats(1, 2)
         bank_stats(1, 3)
         row_stats(1)
-        finish_rows(1)
+        finish_rows(1, 1)
 
-        open_banks(2, psx)
-        chunk_passes(2, 0)
-        chunk_passes(2, 1)
-        turn_and_gate(0, ORDER[:2])
-        chunk_passes(2, 2)
-        turn_and_gate(0, ORDER[2:])
-        chunk_passes(2, 3)
-        leave_psum(2)
-        turn_and_gate(1, ORDER)
         for n in range(N_TILES):
-            bank_stats(2, n)
+            for u in (2, 3):
+                one_bank(u, n)
+                leave_bank(u, n)
+                bank_stats(u, n)
+            if n >= 2:
+                turn_and_gate(n - 2, ORDER)
         row_stats(2)
-        finish_rows(2)
-
-        def chunk_by_chunk(u):
-            open_banks(u, psx)
-            for c in range(PASSES):
-                chunk_passes(u, c)
-
-        bank_by_bank(3)
-        leave_psum(3)
-        turn_and_gate(2, ORDER)
-        for n in range(N_TILES):
-            bank_stats(3, n)
         row_stats(3)
-        finish_rows(3)
+        finish_rows(2, 1)
+        finish_rows(3, 1)
 
-        chunk_by_chunk(4)
+        bank_by_bank(4)
         leave_psum(4)
-        turn_and_gate(3, ORDER)
-        for n in ORDER:
-            multiply(2, n)
+        turn_and_gate(2, ORDER)
         for n in range(N_TILES):
             bank_stats(4, n)
         row_stats(4)
-        finish_rows(4)
+        finish_rows(4, 1)
 
-        bank_by_bank(5)
-        leave_psum(5)
-        turn_and_gate(4, ORDER)
-        for n in range(N_TILES):
-            bank_stats(5, n)
-            multiply(3, ORDER[n])
-        row_stats(5)
-        finish_rows(5)
+        for k in (5, 6):
+            bank_by_bank(k)
+            leave_psum(k)
+            turn_and_gate(k - 2, ORDER)
+            bank_stats(k, 0)
+            multiply(k - 3, 0, 2)
+            bank_stats(k, 1)
+            bank_stats(k, 2)
+            bank_stats(k, 3)
+            row_stats(k)
+            multiply(k - 3, 2, 2)
+            finish_rows(k, 1)
 
-        chunk_by_chunk(6)
-        leave_psum(6)
         bank_by_bank(7)
         leave_psum(7)
-        for n in range(N_TILES):
-            bank_stats(6, n)
-        row_stats(6)
-        finish_rows(6)
         turn_and_gate(5, ORDER)
-        for n in range(N_TILES):
-            turn_back(0, n)
+        turn_and_gate(6, ORDER)
+        turn_back(0, 0)
+        turn_back(0, 1)
         for n in range(N_TILES):
             bank_stats(7, n)
         row_stats(7)
+        finish_rows(7, N_TILES)
         store(0, 0, True)
         store(0, 1, True)
-        finish_rows(7)
-        store(0, 2, True)
-        store(0, 3, True)
-        turn_and_gate(6, ORDER)
         for n in ORDER:
             multiply(6, n)
         turn_and_gate(7, ORDER)
+        turn_back(0, 2)
+        turn_back(0, 3)
+        store(0, 2, True)
+        store(0, 3, True)
         for n in ORDER:
             multiply(7, n)
             turn_back(1, n)

@@ -49,7 +49,7 @@ def tile_dynamicfeaturegroupinglayer_w_e_kernel(
         stage = ctx.enter_context(tc.tile_pool(name="stage", bufs=4))
         wpool = ctx.enter_context(tc.tile_pool(name="wpool", bufs=10))
         zpool = ctx.enter_context(tc.tile_pool(name="zpool", bufs=4))
-        spool = ctx.enter_context(tc.tile_pool(name="spool", bufs=2))
+        spool = ctx.enter_context(tc.tile_pool(name="spool", bufs=4))
         rpool = ctx.enter_context(tc.tile_pool(name="rpool", bufs=4))
         psx = ctx.enter_context(tc.psum_pool(name="psx", bufs=4))
         psy = ctx.enter_context(tc.psum_pool(name="psy", bufs=4))
@@ -402,38 +402,48 @@ def tile_dynamicfeaturegroupinglayer_w_e_kernel(
         row_stats(4)
         finish_rows(4, 1)
 
-        for k in (5, 6):
-            bank_by_bank(k)
-            leave_psum(k)
-            turn_and_gate(k - 2, ORDER)
-            bank_stats(k, 0)
-            multiply(k - 3, 0, 2)
-            bank_stats(k, 1)
-            bank_stats(k, 2)
-            bank_stats(k, 3)
-            row_stats(k)
-            multiply(k - 3, 2, 2)
-            finish_rows(k, 1)
+        for n in range(N_TILES):
+            one_bank(5, n)
+            leave_bank(5, n)
+            if n == 1:
+                turn_and_gate(3, ORDER)
+        turn_and_gate(4, ORDER)
+        bank_stats(5, 0)
+        multiply(2, 0, 2)
+        bank_stats(5, 1)
+        bank_stats(5, 2)
+        bank_stats(5, 3)
+        row_stats(5)
+        multiply(2, 2, 2)
+        finish_rows(5, 1)
+
+        bank_by_bank(6)
+        leave_psum(6)
+        turn_and_gate(5, ORDER)
+        bank_stats(6, 0)
+        multiply(3, 0, 2)
+        bank_stats(6, 1)
+        bank_stats(6, 2)
+        bank_stats(6, 3)
+        row_stats(6)
+        multiply(3, 2, 2)
+        finish_rows(6, 1)
 
         bank_by_bank(7)
         leave_psum(7)
-        turn_and_gate(5, ORDER)
         turn_and_gate(6, ORDER)
-        turn_back(0, 0)
-        turn_back(0, 1)
+        for n in range(N_TILES):
+            turn_back(0, n)
+            store(0, n, False)
         for n in range(N_TILES):
             bank_stats(7, n)
         row_stats(7)
+        multiply(6, 0)
+        multiply(6, 1)
         finish_rows(7, N_TILES)
-        store(0, 0, True)
-        store(0, 1, True)
-        for n in ORDER:
-            multiply(6, n)
+        multiply(6, 2)
+        multiply(6, 3)
         turn_and_gate(7, ORDER)
-        turn_back(0, 2)
-        turn_back(0, 3)
-        store(0, 2, True)
-        store(0, 3, True)
         for n in ORDER:
             multiply(7, n)
             turn_back(1, n)

@@ -115,12 +115,11 @@ def tile_dynamicfeaturegroupinglayer_w_e_kernel(
             return tiles
 
         loaded = {}
-        load_scales(0, 0)
+        for g in range(GROUPS):
+            for v in range(2):
+                load_scales(g, v)
         loaded[(0, 0)] = load_words(0, 0)
-        load_scales(0, 1)
         loaded[(0, 1)] = load_columns(0, 1)
-        load_scales(1, 0)
-        load_scales(1, 1)
         loaded[(1, 0)] = load_columns(1, 0)
 
         a_codes = keep.tile([P, GROUPS * PASSES, MASKS * P], U32, align_bytes=64)

@@ -54,6 +54,8 @@ def tile_dynamicfeaturegroupinglayer_w_e_kernel(
         psx = ctx.enter_context(tc.psum_pool(name="psx", bufs=4))
         psy = ctx.enter_context(tc.psum_pool(name="psy", bufs=4))
 
+        wrow = keep.tile([P, K_PASS], BF16)
+        nc.vector.memset(wrow[:].bitcast(I32), 0)
         planes = keep.tile([P, 2 * GROUPS, H], U8, align_bytes=64)
         nc.vector.memset(planes[:].rearrange("p f n -> p (f n)").bitcast(I32), 0)
         ones = keep.tile([P, P], F32)
@@ -69,10 +71,8 @@ def tile_dynamicfeaturegroupinglayer_w_e_kernel(
 
         wc = keep.tile([P, S // CHUNKS], BF16)
         nc.sync.dma_start(out=wc[:], in_=W_masks.rearrange("g m (i f) -> (g m i) f", i=CHUNKS))
-        wm = keep.tile([P, ROWS, TAPS], BF16)
         nc.sync.dma_start(
-            out=wm[:].rearrange("p a (c t) -> p (a c) t", t=PACK),
-            in_=W_masks.rearrange("g m (c p t) -> p (g m c) t", c=PASSES, p=P, t=PACK),
+            out=wrow[0 : ROWS * PASSES, :], in_=W_masks.rearrange("g m (c k) -> (g m c) k", c=PASSES)
         )
         x_sb = keep.tile([P, GROUPS * S], BF16)
         for g in range(GROUPS):
@@ -171,10 +171,17 @@ def tile_dynamicfeaturegroupinglayer_w_e_kernel(
         )
         neg_top = small.tile([P, ROWS], F32)
         nc.vector.tensor_reduce(out=neg_top[:], in_=tops[:], axis=AX.X, op=ALU.max, negate=True)
+        wt = psx.tile([P, 2, P], F32, tag="bank")
+        for u in range(2):
+            nc.tensor.transpose(wt[:, u, :], wrow[:].bitcast(F32)[:, u : K_PASS // 2 : 2], ident_f[:])
         shifted = small.tile([P, ROWS, TAPS], F32)
-        nc.vector.tensor_tensor(
-            out=shifted[:], in0=wm[:], in1=neg_top[:].unsqueeze(2).to_broadcast([P, ROWS, TAPS]), op=ALU.add
-        )
+        for u in range(2):
+            nc.vector.tensor_tensor(
+                out=shifted[:].rearrange("p a (c u e) -> p a c u e", u=2, e=2)[:, :, :, u, :],
+                in0=wt[:, u, 0 : ROWS * PASSES].bitcast(BF16).rearrange("p (a c e) -> p a c e", c=PASSES, e=2),
+                in1=neg_top[:].unsqueeze(2).unsqueeze(3).to_broadcast([P, ROWS, PASSES, 2]),
+                op=ALU.add,
+            )
         powered = small.tile([P, ROWS, TAPS], F32)
         nc.scalar.activation(
             out=powered[:].rearrange("p a t -> p (a t)"),

@@ -288,9 +288,7 @@ def tile_dynamicfeaturegroupinglayer_w_e_kernel(
             mv = small.tile([P, 2], F32, name="mv")
             nc.vector.bn_aggr(out=mv[:], in_=stats_of[u][:].rearrange("p n s -> p (n s)"))
             var_eps = small.tile([P, 1], F32, name="var_eps")
-            nc.gpsimd.tensor_scalar(
-                out=var_eps[:], in0=mv[:, 1:2], scalar1=1.0, scalar2=EPS, op0=ALU.mult, op1=ALU.add
-            )
+            nc.vector.tensor_scalar_add(out=var_eps[:], in0=mv[:, 1:2], scalar1=EPS)
             rstd = small.tile([P, 1], F32, name="rstd")
             nc.gpsimd.tensor_tensor(out=rstd[:], in0=var_eps[:], in1=neg_half[:], op=ALU.pow)
             mv_of[u], rstd_of[u] = mv, rstd
@@ -417,10 +415,10 @@ def tile_dynamicfeaturegroupinglayer_w_e_kernel(
         bank_stats(5, 0)
         multiply(2, 0, 2)
         bank_stats(5, 1)
+        multiply(2, 2, 2)
         bank_stats(5, 2)
         bank_stats(5, 3)
         row_stats(5)
-        multiply(2, 2, 2)
         finish_rows(5, 1)
 
         bank_by_bank(6)
@@ -429,10 +427,10 @@ def tile_dynamicfeaturegroupinglayer_w_e_kernel(
         bank_stats(6, 0)
         multiply(3, 0, 2)
         bank_stats(6, 1)
+        multiply(3, 2, 2)
         bank_stats(6, 2)
         bank_stats(6, 3)
         row_stats(6)
-        multiply(3, 2, 2)
         finish_rows(6, 1)
 
         bank_by_bank(7)
@@ -444,11 +442,9 @@ def tile_dynamicfeaturegroupinglayer_w_e_kernel(
         for n in range(N_TILES):
             bank_stats(7, n)
         row_stats(7)
-        multiply(6, 0)
-        multiply(6, 1)
         finish_rows(7, N_TILES)
-        multiply(6, 2)
-        multiply(6, 3)
+        for n in ORDER:
+            multiply(6, n)
         turn_and_gate(7, ORDER)
         for n in ORDER:
             multiply(7, n)

@@ -120,7 +120,7 @@ def tile_dynamicfeaturegroupinglayer_w_e_kernel(
                 load_scales(g, v)
         loaded[(0, 0)] = load_words(0, 0)
         loaded[(0, 1)] = load_columns(0, 1)
-        loaded[(1, 0)] = load_columns(1, 0)
+        loaded[(1, 0)] = load_words(1, 0)
 
         a_codes = keep.tile([P, GROUPS * PASSES, MASKS * P], U32, align_bytes=64)
         a_scales = keep.tile([P, GROUPS * PASSES, MASKS * P], U8, align_bytes=64)
@@ -237,7 +237,7 @@ def tile_dynamicfeaturegroupinglayer_w_e_kernel(
                 out=banks_of[u][n][:],
                 lhsT=a_codes[:, gp, m * P : (m + 1) * P].bitcast(FP8X4),
                 lhsT_scale=a_scales[:, gp, m * P : (m + 1) * P],
-                rhs=(loaded[(g, v)][c][:, cols] if (g, v) == (0, 0) else loaded[(g, v)][n][:, c, :]).bitcast(FP8X4),
+                rhs=(loaded[(g, v)][n][:, c, :] if (g, v) == (0, 1) else loaded[(g, v)][c][:, cols]).bitcast(FP8X4),
                 rhs_scale=planes[4 * c : P, 2 * g + v, cols],
                 start=(c == 0),
                 stop=(c == PASSES - 1),
@@ -372,7 +372,7 @@ def tile_dynamicfeaturegroupinglayer_w_e_kernel(
         for c in range(PASSES):
             chunk_passes(0, c)
             chunk_passes(1, c)
-        loaded[(1, 1)] = load_columns(1, 1)
+        loaded[(1, 1)] = load_words(1, 1)
         leave_psum(0)
         leave_psum(1)
         for n in range(N_TILES):
@@ -398,7 +398,9 @@ def tile_dynamicfeaturegroupinglayer_w_e_kernel(
         finish_rows(2, 1)
         finish_rows(3, 1)
 
-        bank_by_bank(4)
+        open_banks(4, psx)
+        for c in range(PASSES):
+            chunk_passes(4, c)
         leave_psum(4)
         turn_and_gate(2, ORDER)
         for n in range(N_TILES):

@@ -70,19 +70,8 @@ def tile_dynamicfeaturegroupinglayer_w_e_kernel(
         make_identity(nc, ident_b[:])
 
         wc = keep.tile([P, S // CHUNKS], BF16)
-        nc.sync.dma_start(out=wc[:], in_=W_masks.rearrange("g m (i f) -> (g m i) f", i=CHUNKS))
-        nc.sync.dma_start(
-            out=wrow[0 : ROWS * PASSES, :], in_=W_masks.rearrange("g m (c k) -> (g m c) k", c=PASSES)
-        )
         x_sb = keep.tile([P, GROUPS * S], BF16)
-        for g in range(GROUPS):
-            nc.sync.dma_start(out=x_sb[:, g * S : (g + 1) * S], in_=x[:, g * S : (g + 1) * S])
-        prm = keep.tile([P, P], BF16)
-        for r in range(4):
-            nc.scalar.dma_start(
-                out=prm[32 * r : 32 * (r + 1), :], in_=ln_rows[r].rearrange("g (jt p) -> (g jt) p", p=P)
-            )
-
+        loaded = {}
         def load_scales(g, v):
             for q in range(4):
                 nc.sync.dma_start(
@@ -90,37 +79,45 @@ def tile_dynamicfeaturegroupinglayer_w_e_kernel(
                     in_=w_scales[v][PASSES * g : PASSES * (g + 1), 4 * q : 4 * q + 4, :].bitcast(I32),
                 )
 
-        def load_words(g, v):
-            chunks = []
-            for c in range(PASSES):
-                chunk = wpool.tile([P, H], U32, name="chunk", align_bytes=64)
-                nc.sync.dma_start(
-                    out=chunk[:].bitcast(I32),
-                    in_=w_words[v][PASSES * g + c].rearrange("p n t -> p (n t)").bitcast(I32),
-                )
-                chunks.append(chunk)
-            return chunks
+        def load_pass(g, v, c):
+            chunk = wpool.tile([P, H], U32, name="chunk", align_bytes=64)
+            nc.sync.dma_start(
+                out=chunk[:].bitcast(I32),
+                in_=w_words[v][PASSES * g + c].rearrange("p n t -> p (n t)").bitcast(I32),
+            )
+            loaded.setdefault((g, v), []).append(chunk)
 
-        def load_columns(g, v):
-            tiles = []
-            for n in range(N_TILES):
-                chunk = wpool.tile([P, PASSES, N_TILE], U32, name="chunk", align_bytes=64)
-                nc.sync.dma_start(
-                    out=chunk[:].bitcast(I32),
-                    in_=w_words[v][PASSES * g : PASSES * (g + 1), :, n * N_TILE : (n + 1) * N_TILE, :]
-                    .rearrange("c p n t -> p c (n t)")
-                    .bitcast(I32),
-                )
-                tiles.append(chunk)
-            return tiles
+        def load_columns(g, v, n):
+            chunk = wpool.tile([P, PASSES, N_TILE], U32, name="chunk", align_bytes=64)
+            nc.sync.dma_start(
+                out=chunk[:].bitcast(I32),
+                in_=w_words[v][PASSES * g : PASSES * (g + 1), :, n * N_TILE : (n + 1) * N_TILE, :]
+                .rearrange("c p n t -> p c (n t)")
+                .bitcast(I32),
+            )
+            loaded.setdefault((g, v), []).append(chunk)
 
-        loaded = {}
-        for g in range(GROUPS):
-            for v in range(2):
-                load_scales(g, v)
-        loaded[(0, 0)] = load_words(0, 0)
-        loaded[(0, 1)] = load_columns(0, 1)
-        loaded[(1, 0)] = load_words(1, 0)
+        nc.sync.dma_start(out=wc[:], in_=W_masks.rearrange("g m (i f) -> (g m i) f", i=CHUNKS))
+        nc.sync.dma_start(
+            out=wrow[0 : ROWS * PASSES, :], in_=W_masks.rearrange("g m (c k) -> (g m c) k", c=PASSES)
+        )
+        nc.sync.dma_start(out=x_sb[:], in_=x)
+        load_scales(0, 0)
+        load_pass(0, 0, 0)
+        load_pass(0, 0, 1)
+        load_pass(0, 0, 2)
+        load_pass(0, 0, 3)
+        load_scales(0, 1)
+        load_columns(0, 1, 0)
+        load_columns(0, 1, 1)
+        load_columns(0, 1, 2)
+        load_columns(0, 1, 3)
+        load_scales(1, 0)
+        load_pass(1, 0, 0)
+        load_pass(1, 0, 1)
+        load_pass(1, 0, 2)
+        load_pass(1, 0, 3)
+        load_scales(1, 1)
 
         a_codes = keep.tile([P, GROUPS * PASSES, MASKS * P], U32, align_bytes=64)
         a_scales = keep.tile([P, GROUPS * PASSES, MASKS * P], U8, align_bytes=64)
@@ -207,15 +204,17 @@ def tile_dynamicfeaturegroupinglayer_w_e_kernel(
         )
         for pair in range(1, GROUPS * PASSES // 2):
             x_banks.append(turn_x(pair))
-        prm_ps = psx.tile([P, P], BF16, tag="bank")
-        nc.tensor.transpose(prm_ps[:], prm[:], ident_b[:])
         warm = small.tile([P, 1], F32)
         for pair in range(GROUPS * PASSES // 2):
             nc.scalar.copy(out=x_words[:, 2 * pair : 2 * pair + 2], in_=x_banks[pair][:])
             if pair == 1:
                 nc.scalar.activation(out=warm[:], in_=neg_half[:], func=ACT.Sigmoid)
-        prm_t = keep.tile([P, P], F32)
-        nc.scalar.copy(out=prm_t[:], in_=prm_ps[:])
+        prm = keep.tile([P, P], BF16)
+        for r in range(4):
+            nc.scalar.dma_start(
+                out=prm[32 * r : 32 * (r + 1), :], in_=ln_rows[r].rearrange("g (jt p) -> (g jt) p", p=P)
+            )
+
 
         units = [(g, v, m) for g in range(GROUPS) for v in range(2) for m in range(MASKS)]
         n_units = len(units)
@@ -372,8 +371,13 @@ def tile_dynamicfeaturegroupinglayer_w_e_kernel(
         for c in range(PASSES):
             chunk_passes(0, c)
             chunk_passes(1, c)
-        loaded[(1, 1)] = load_words(1, 1)
+        for c in range(PASSES):
+            load_pass(1, 1, c)
         leave_psum(0)
+        prm_ps = psx.tile([P, P], BF16, tag="bank")
+        nc.tensor.transpose(prm_ps[:], prm[:], ident_b[:])
+        prm_t = keep.tile([P, P], F32)
+        nc.scalar.copy(out=prm_t[:], in_=prm_ps[:])
         leave_psum(1)
         for n in range(N_TILES):
             bank_stats(0, n)

@@ -357,6 +357,11 @@ def tile_dynamicfeaturegroupinglayer_w_e_kernel(
                 nc.scalar.copy(out=result[:], in_=back_of[(g, n)][:].rearrange("p j b -> p (j b)"))
             nc.sync.dma_start(out=out[:, g * H + n * N_TILE : g * H + (n + 1) * N_TILE], in_=result[:])
 
+        def keep_warm(passes):
+            idle = psx.tile([P, N_TILE], F32, name="idle", tag="bank")
+            for i in range(passes):
+                nc.tensor.matmul(out=idle[:], lhsT=ident_b[:], rhs=x_sb[:, 0:N_TILE], start=True, stop=True)
+
         weigh(0, True)
         previous = None
         for gp in range(1, GROUPS * PASSES):
@@ -442,9 +447,12 @@ def tile_dynamicfeaturegroupinglayer_w_e_kernel(
         bank_by_bank(7)
         leave_psum(7)
         turn_and_gate(6, ORDER)
+        keep_warm(2)
         for n in range(N_TILES):
             turn_back(0, n)
             store(0, n, False)
+            if n == 1:
+                keep_warm(2)
         for n in range(N_TILES):
             bank_stats(7, n)
         row_stats(7)
@@ -452,6 +460,7 @@ def tile_dynamicfeaturegroupinglayer_w_e_kernel(
         for n in ORDER:
             multiply(6, n)
         turn_and_gate(7, ORDER)
+        keep_warm(6)
         for n in ORDER:
             multiply(7, n)
             turn_back(1, n)

@@ -188,27 +188,38 @@ def tile_dynamicfeaturegroupinglayer_w_e_kernel(
         )
         part = small.tile([P, ROWS], F32)
         nc.vector.tensor_reduce(out=part[:], in_=powered[:], axis=AX.X, op=ALU.add)
-        x_banks = [turn_x(0)]
         total_ps = psx.tile([P, ROWS], F32, tag="bank")
         nc.tensor.matmul(out=total_ps[:], lhsT=ones[:], rhs=part[:], start=True, stop=True)
+        x_banks = [turn_x(0)]
         e = small.tile([P, ROWS, TAPS], F32)
         nc.scalar.activation(
             out=e[:].rearrange("p a t -> p (a t)"), in_=shifted[:].rearrange("p a t -> p (a t)"), func=ACT.Exp
         )
         total = small.tile([P, ROWS], F32)
         nc.vector.tensor_scalar_add(out=total[:], in0=total_ps[:], scalar1=EPS)
-        inv_norm = small.tile([P, ROWS], F32)
-        nc.gpsimd.tensor_tensor(out=inv_norm[:], in0=total[:], in1=exponent[:], op=ALU.pow)
-        nc.vector.tensor_tensor(
-            out=mask[:], in0=e[:], in1=inv_norm[:].unsqueeze(2).to_broadcast([P, ROWS, TAPS]), op=ALU.mult
-        )
+        inv_norms = []
+        for g in range(GROUPS):
+            rows = slice(MASKS * g, MASKS * (g + 1))
+            inv_norm = small.tile([P, MASKS], F32, name="inv_norm")
+            nc.gpsimd.tensor_tensor(out=inv_norm[:], in0=total[:, rows], in1=exponent[:, rows], op=ALU.pow)
+            inv_norms.append(inv_norm)
+
+        def finish_mask(g):
+            rows = slice(MASKS * g, MASKS * (g + 1))
+            nc.vector.tensor_tensor(
+                out=mask[:, rows, :],
+                in0=e[:, rows, :],
+                in1=inv_norms[g][:].unsqueeze(2).to_broadcast([P, MASKS, TAPS]),
+                op=ALU.mult,
+            )
+
+        finish_mask(0)
         for pair in range(1, GROUPS * PASSES // 2):
             x_banks.append(turn_x(pair))
         warm = small.tile([P, 1], F32)
         for pair in range(GROUPS * PASSES // 2):
             nc.scalar.copy(out=x_words[:, 2 * pair : 2 * pair + 2], in_=x_banks[pair][:])
-            if pair == 1:
-                nc.scalar.activation(out=warm[:], in_=neg_half[:], func=ACT.Sigmoid)
+        nc.scalar.activation(out=warm[:], in_=neg_half[:], func=ACT.Sigmoid)
         prm = keep.tile([P, P], BF16)
         for r in range(4):
             nc.scalar.dma_start(
@@ -363,6 +374,7 @@ def tile_dynamicfeaturegroupinglayer_w_e_kernel(
                 nc.tensor.matmul(out=idle[:], lhsT=ident_b[:], rhs=x_sb[:, 0:N_TILE], start=True, stop=True)
 
         weigh(0, True)
+        finish_mask(1)
         previous = None
         for gp in range(1, GROUPS * PASSES):
             grouped = weigh(gp, False)
@@ -457,8 +469,8 @@ def tile_dynamicfeaturegroupinglayer_w_e_kernel(
             bank_stats(7, n)
         row_stats(7)
         finish_rows(7, N_TILES)
-        for n in ORDER:
-            multiply(6, n)
+        multiply(6, 0, 2)
+        multiply(6, 2, 2)
         turn_and_gate(7, ORDER)
         keep_warm(6)
         for n in ORDER:

@@ -97,6 +97,16 @@ def tile_dynamicfeaturegroupinglayer_w_e_kernel(
             )
             loaded.setdefault((g, v), []).append(chunk)
 
+        def load_half(g, v, h, d):
+            chunk = wpool.tile([P, 2, H // 2], U32, name="chunk", align_bytes=64)
+            nc.sync.dma_start(
+                out=chunk[:].bitcast(I32),
+                in_=w_words[v][PASSES * g + 2 * d : PASSES * g + 2 * d + 2, :, h * H // 2 : (h + 1) * H // 2, :]
+                .rearrange("c p n t -> p c (n t)")
+                .bitcast(I32),
+            )
+            loaded.setdefault((g, v), []).append(chunk)
+
         nc.sync.dma_start(out=wc[:], in_=W_masks.rearrange("g m (i f) -> (g m i) f", i=CHUNKS))
         nc.sync.dma_start(
             out=wrow[0 : ROWS * PASSES, :], in_=W_masks.rearrange("g m (c k) -> (g m c) k", c=PASSES)
@@ -239,6 +249,14 @@ def tile_dynamicfeaturegroupinglayer_w_e_kernel(
                 acc = pool.tile([P, N_TILE], F32, name="acc", tag="bank")
                 banks_of[u].append(acc)
 
+        def words(g, v, c, n):
+            tiles = loaded[(g, v)]
+            if (g, v) == (0, 1):
+                return tiles[n][:, c, :]
+            if (g, v) == (1, 1):
+                return tiles[2 * (n // 2) + c // 2][:, c % 2, n % 2 * N_TILE : (n % 2 + 1) * N_TILE]
+            return tiles[c][:, n * N_TILE : (n + 1) * N_TILE]
+
         def one_pass(u, c, n):
             g, v, m = units[u]
             gp = PASSES * g + c
@@ -247,7 +265,7 @@ def tile_dynamicfeaturegroupinglayer_w_e_kernel(
                 out=banks_of[u][n][:],
                 lhsT=a_codes[:, gp, m * P : (m + 1) * P].bitcast(FP8X4),
                 lhsT_scale=a_scales[:, gp, m * P : (m + 1) * P],
-                rhs=(loaded[(g, v)][n][:, c, :] if (g, v) == (0, 1) else loaded[(g, v)][c][:, cols]).bitcast(FP8X4),
+                rhs=words(g, v, c, n).bitcast(FP8X4),
                 rhs_scale=planes[4 * c : P, 2 * g + v, cols],
                 start=(c == 0),
                 stop=(c == PASSES - 1),
@@ -389,7 +407,7 @@ def tile_dynamicfeaturegroupinglayer_w_e_kernel(
             chunk_passes(0, c)
             chunk_passes(1, c)
         for c in range(PASSES):
-            load_pass(1, 1, c)
+            load_half(1, 1, c // 2, c % 2)
         leave_psum(0)
         prm_ps = psx.tile([P, P], BF16, tag="bank")
         nc.tensor.transpose(prm_ps[:], prm[:], ident_b[:])
@@ -472,7 +490,7 @@ def tile_dynamicfeaturegroupinglayer_w_e_kernel(
         multiply(6, 0, 2)
         multiply(6, 2, 2)
         turn_and_gate(7, ORDER)
-        keep_warm(6)
+        keep_warm(3)
         for n in ORDER:
             multiply(7, n)
             turn_back(1, n)

from contextlib import ExitStack

import concourse.mybir as mybir
from concourse.masks import make_identity

F32 = mybir.dt.float32
BF16 = mybir.dt.bfloat16
I32 = mybir.dt.int32
U32 = mybir.dt.uint32
U8 = mybir.dt.uint8
FP8X4 = mybir.dt.float8_e4m3fn_x4
ALU = mybir.AluOpType
ACT = mybir.ActivationFunctionType
AX = mybir.AxisListType

P = 128
GROUPS = 2
MASKS = 2
S = 2048
H = 2048
PACK = 4
K_PASS = P * PACK
PASSES = S // K_PASS
N_TILE = 512
N_TILES = H // N_TILE
J_TILES = H // P
J_BANK = N_TILE // P
ROWS = GROUPS * MASKS
TAPS = PASSES * PACK
ALPHA = 1.1
EPS = 1e-5
CHUNKS = P // ROWS

FLOPS = 2 * P * GROUPS * MASKS * S * H * 2


def tile_dynamicfeaturegroupinglayer_w_e_kernel(
    tc, x, W_masks, W1_words, W1_scales, W2_words, W2_scales, ln1_w, ln1_b, ln2_w, ln2_b, out
):
    nc = tc.nc
    w_words = (W1_words, W2_words)
    w_scales = (W1_scales, W2_scales)
    ln_rows = (ln1_w, ln1_b, ln2_w, ln2_b)

    with ExitStack() as ctx:
        ctx.enter_context(tc.manual_schedule())
        keep = ctx.enter_context(tc.tile_pool(name="keep", bufs=1))
        small = ctx.enter_context(tc.tile_pool(name="small", bufs=4))
        stage = ctx.enter_context(tc.tile_pool(name="stage", bufs=4))
        wpool = ctx.enter_context(tc.tile_pool(name="wpool", bufs=10))
        zpool = ctx.enter_context(tc.tile_pool(name="zpool", bufs=4))
        spool = ctx.enter_context(tc.tile_pool(name="spool", bufs=4))
        rpool = ctx.enter_context(tc.tile_pool(name="rpool", bufs=4))
        psx = ctx.enter_context(tc.psum_pool(name="psx", bufs=4))
        psy = ctx.enter_context(tc.psum_pool(name="psy", bufs=4))

        wrow = keep.tile([P, K_PASS], BF16)
        nc.vector.memset(wrow[:].bitcast(I32), 0)
        planes = keep.tile([P, 2 * GROUPS, H], U8, align_bytes=64)
        nc.vector.memset(planes[:].rearrange("p f n -> p (f n)").bitcast(I32), 0)
        ones = keep.tile([P, P], F32)
        nc.vector.memset(ones[:], 1.0)
        exponent = keep.tile([P, ROWS], F32)
        nc.vector.tensor_scalar_mul(out=exponent[:], in0=ones[:, 0:ROWS], scalar1=-1.0 / ALPHA)
        neg_half = keep.tile([P, 1], F32)
        nc.vector.memset(neg_half[:], -0.5)
        ident_f = keep.tile([P, P], F32)
        make_identity(nc, ident_f[:])
        ident_b = keep.tile([P, P], BF16)
        make_identity(nc, ident_b[:])

        wc = keep.tile([P, S // CHUNKS], BF16)
        x_sb = keep.tile([P, GROUPS * S], BF16)
        loaded = {}
        def load_scales(g, v):
            for q in range(4):
                nc.sync.dma_start(
                    out=planes[32 * q : 32 * q + 16, 2 * g + v, :].bitcast(I32),
                    in_=w_scales[v][PASSES * g : PASSES * (g + 1), 4 * q : 4 * q + 4, :].bitcast(I32),
                )

        def load_pass(g, v, c):
            chunk = wpool.tile([P, H], U32, name="chunk", align_bytes=64)
            nc.sync.dma_start(
                out=chunk[:].bitcast(I32),
                in_=w_words[v][PASSES * g + c].rearrange("p n t -> p (n t)").bitcast(I32),
            )
            loaded.setdefault((g, v), []).append(chunk)

        def load_columns(g, v, n):
            chunk = wpool.tile([P, PASSES, N_TILE], U32, name="chunk", align_bytes=64)
            nc.sync.dma_start(
                out=chunk[:].bitcast(I32),
                in_=w_words[v][PASSES * g : PASSES * (g + 1), :, n * N_TILE : (n + 1) * N_TILE, :]
                .rearrange("c p n t -> p c (n t)")
                .bitcast(I32),
            )
            loaded.setdefault((g, v), []).append(chunk)

        def load_half(g, v, h, d):
            chunk = wpool.tile([P, 2, H // 2], U32, name="chunk", align_bytes=64)
            nc.sync.dma_start(
                out=chunk[:].bitcast(I32),
                in_=w_words[v][PASSES * g + 2 * d : PASSES * g + 2 * d + 2, :, h * H // 2 : (h + 1) * H // 2, :]
                .rearrange("c p n t -> p c (n t)")
                .bitcast(I32),
            )
            loaded.setdefault((g, v), []).append(chunk)

        nc.sync.dma_start(out=wc[:], in_=W_masks.rearrange("g m (i f) -> (g m i) f", i=CHUNKS))
        nc.sync.dma_start(
            out=wrow[0 : ROWS * PASSES, :], in_=W_masks.rearrange("g m (c k) -> (g m c) k", c=PASSES)
        )
        nc.sync.dma_start(out=x_sb[:], in_=x)
        load_scales(0, 0)
        load_pass(0, 0, 0)
        load_pass(0, 0, 1)
        load_pass(0, 0, 2)
        load_pass(0, 0, 3)
        load_scales(0, 1)
        load_columns(0, 1, 0)
        load_columns(0, 1, 1)
        load_columns(0, 1, 2)
        load_columns(0, 1, 3)
        load_scales(1, 0)
        load_pass(1, 0, 0)
        load_pass(1, 0, 1)
        load_pass(1, 0, 2)
        load_pass(1, 0, 3)
        load_scales(1, 1)

        a_codes = keep.tile([P, GROUPS * PASSES, MASKS * P], U32, align_bytes=64)
        a_scales = keep.tile([P, GROUPS * PASSES, MASKS * P], U8, align_bytes=64)
        x_pairs = x_sb[:].bitcast(F32)
        mask = keep.tile([P, ROWS, TAPS], F32)
        x_words = keep.tile([P, GROUPS * PASSES, 2, P], F32)

        def turn_x(pair):
            xt = psy.tile([P, 2, 2, P], F32, name="xt", tag="bank")
            for i in range(2):
                gp = 2 * pair + i
                for u in range(2):
                    nc.tensor.transpose(xt[:, i, u, :], x_pairs[:, 256 * gp + u : 256 * (gp + 1) : 2], ident_f[:])
            return xt

        def weigh(gp, at_once):
            grouped = stage.tile([P, MASKS, P, PACK], BF16, name="grouped", align_bytes=64)
            for m in range(MASKS):
                nc.vector.tensor_tensor(
                    out=grouped[:, m].rearrange("p b (u e) -> p b u e", e=2),
                    in0=x_words[:, gp].bitcast(BF16).rearrange("p u (b e) -> p b u e", e=2),
                    in1=mask[:, MASKS * (gp // PASSES) + m, PACK * (gp % PASSES) : PACK * (gp % PASSES + 1)]
                    .rearrange("p (u e) -> p u e", e=2)
                    .unsqueeze(1)
                    .to_broadcast([P, P, 2, 2]),
                    op=ALU.mult,
                )
                if at_once:
                    nc.vector.quantize_mx(
                        out=a_codes[:, gp, m * P : (m + 1) * P].bitcast(FP8X4),
                        scales=a_scales[:, gp, m * P : (m + 1) * P],
                        in_=grouped[:, m].rearrange("p b t -> p (b t)"),
                    )
            return grouped

        def quantise(gp, grouped):
            nc.vector.quantize_mx(
                out=a_codes[:, gp, :].bitcast(FP8X4),
                scales=a_scales[:, gp, :],
                in_=grouped[:].rearrange("p m b t -> p (m b t)"),
            )

        piece_top = small.tile([P, 1], F32)
        nc.vector.tensor_reduce(out=piece_top[:], in_=wc[:], axis=AX.X, op=ALU.max)
        tops = psx.tile([P, ROWS, CHUNKS], F32, tag="bank")
        nc.tensor.transpose(
            tops[:].rearrange("p a i -> p (a i)"), piece_top[:, 0:1].to_broadcast([P, P]), ident_f[:]
        )
        neg_top = small.tile([P, ROWS], F32)
        nc.vector.tensor_reduce(out=neg_top[:], in_=tops[:], axis=AX.X, op=ALU.max, negate=True)
        wt = psx.tile([P, 2, P], F32, tag="bank")
        for u in range(2):
            nc.tensor.transpose(wt[:, u, :], wrow[:].bitcast(F32)[:, u : K_PASS // 2 : 2], ident_f[:])
        shifted = small.tile([P, ROWS, TAPS], F32)
        for u in range(2):
            nc.vector.tensor_tensor(
                out=shifted[:].rearrange("p a (c u e) -> p a c u e", u=2, e=2)[:, :, :, u, :],
                in0=wt[:, u, 0 : ROWS * PASSES].bitcast(BF16).rearrange("p (a c e) -> p a c e", c=PASSES, e=2),
                in1=neg_top[:].unsqueeze(2).unsqueeze(3).to_broadcast([P, ROWS, PASSES, 2]),
                op=ALU.add,
            )
        powered = small.tile([P, ROWS, TAPS], F32)
        nc.scalar.activation(
            out=powered[:].rearrange("p a t -> p (a t)"),
            in_=shifted[:].rearrange("p a t -> p (a t)"),
            func=ACT.Exp,
            scale=ALPHA,
        )
        part = small.tile([P, ROWS], F32)
        nc.vector.tensor_reduce(out=part[:], in_=powered[:], axis=AX.X, op=ALU.add)
        total_ps = psx.tile([P, ROWS], F32, tag="bank")
        nc.tensor.matmul(out=total_ps[:], lhsT=ones[:], rhs=part[:], start=True, stop=True)
        x_banks = [turn_x(0)]
        e = small.tile([P, ROWS, TAPS], F32)
        nc.scalar.activation(
            out=e[:].rearrange("p a t -> p (a t)"), in_=shifted[:].rearrange("p a t -> p (a t)"), func=ACT.Exp
        )
        total = small.tile([P, ROWS], F32)
        nc.vector.tensor_scalar_add(out=total[:], in0=total_ps[:], scalar1=EPS)
        inv_norms = []
        for g in range(GROUPS):
            rows = slice(MASKS * g, MASKS * (g + 1))
            inv_norm = small.tile([P, MASKS], F32, name="inv_norm")
            nc.gpsimd.tensor_tensor(out=inv_norm[:], in0=total[:, rows], in1=exponent[:, rows], op=ALU.pow)
            inv_norms.append(inv_norm)

        def finish_mask(g):
            rows = slice(MASKS * g, MASKS * (g + 1))
            nc.vector.tensor_tensor(
                out=mask[:, rows, :],
                in0=e[:, rows, :],
                in1=inv_norms[g][:].unsqueeze(2).to_broadcast([P, MASKS, TAPS]),
                op=ALU.mult,
            )

        finish_mask(0)
        for pair in range(1, GROUPS * PASSES // 2):
            x_banks.append(turn_x(pair))
        warm = small.tile([P, 1], F32)
        for pair in range(GROUPS * PASSES // 2):
            nc.scalar.copy(out=x_words[:, 2 * pair : 2 * pair + 2], in_=x_banks[pair][:])
        nc.scalar.activation(out=warm[:], in_=neg_half[:], func=ACT.Sigmoid)
        prm = keep.tile([P, P], BF16)
        for r in range(4):
            nc.scalar.dma_start(
                out=prm[32 * r : 32 * (r + 1), :], in_=ln_rows[r].rearrange("g (jt p) -> (g jt) p", p=P)
            )


        units = [(g, v, m) for g in range(GROUPS) for v in range(2) for m in range(MASKS)]
        n_units = len(units)
        banks_of, mv_of, rstd_of, z_of, zt_of, gate_of, stats_of = {}, {}, {}, {}, {}, {}, {}
        back_of = {}
        ORDER = (0, 1, 2, 3)

        def open_banks(u, pool):
            banks_of[u] = []
            for n in range(N_TILES):
                acc = pool.tile([P, N_TILE], F32, name="acc", tag="bank")
                banks_of[u].append(acc)

        def words(g, v, c, n):
            tiles = loaded[(g, v)]
            if (g, v) == (0, 1):
                return tiles[n][:, c, :]
            if (g, v) == (1, 1):
                return tiles[2 * (n // 2) + c // 2][:, c % 2, n % 2 * N_TILE : (n % 2 + 1) * N_TILE]
            return tiles[c][:, n * N_TILE : (n + 1) * N_TILE]

        def one_pass(u, c, n):
            g, v, m = units[u]
            gp = PASSES * g + c
            cols = slice(n * N_TILE, (n + 1) * N_TILE)
            nc.tensor.matmul_mx(
                out=banks_of[u][n][:],
                lhsT=a_codes[:, gp, m * P : (m + 1) * P].bitcast(FP8X4),
                lhsT_scale=a_scales[:, gp, m * P : (m + 1) * P],
                rhs=words(g, v, c, n).bitcast(FP8X4),
                rhs_scale=planes[4 * c : P, 2 * g + v, cols],
                start=(c == 0),
                stop=(c == PASSES - 1),
            )

        def chunk_passes(u, c):
            for n in range(N_TILES):
                one_pass(u, c, n)

        def one_bank(u, n):
            acc = psx.tile([P, N_TILE], F32, name="acc", tag="bank")
            banks_of.setdefault(u, []).append(acc)
            for c in range(PASSES):
                one_pass(u, c, n)

        def bank_by_bank(u):
            for n in range(N_TILES):
                one_bank(u, n)

        def leave_bank(u, n):
            if n == 0:
                z = zpool.tile([P, H], F32, name="z")
                z_of[u] = z
            nc.scalar.copy(out=z_of[u][:, n * N_TILE : (n + 1) * N_TILE], in_=banks_of[u][n][:])

        def leave_psum(u):
            for n in range(N_TILES):
                leave_bank(u, n)

        def bank_stats(u, n):
            if n == 0:
                stats = small.tile([P, N_TILES, 6], F32, name="stats")
                stats_of[u] = stats
            nc.vector.bn_stats(out=stats_of[u][:, n, :], in_=z_of[u][:, n * N_TILE : (n + 1) * N_TILE])

        def normalise(u, first, banks):
            cols = slice(first * N_TILE, (first + banks) * N_TILE)
            nc.vector.tensor_scalar(
                out=z_of[u][:, cols],
                in0=z_of[u][:, cols],
                scalar1=mv_of[u][:, 0:1],
                scalar2=rstd_of[u][:, 0:1],
                op0=ALU.subtract,
                op1=ALU.mult,
            )

        def row_stats(u):
            mv = small.tile([P, 2], F32, name="mv")
            nc.vector.bn_aggr(out=mv[:], in_=stats_of[u][:].rearrange("p n s -> p (n s)"))
            var_eps = small.tile([P, 1], F32, name="var_eps")
            nc.vector.tensor_scalar_add(out=var_eps[:], in0=mv[:, 1:2], scalar1=EPS)
            rstd = small.tile([P, 1], F32, name="rstd")
            nc.gpsimd.tensor_tensor(out=rstd[:], in0=var_eps[:], in1=neg_half[:], op=ALU.pow)
            mv_of[u], rstd_of[u] = mv, rstd

        def finish_rows(u, pieces):
            for i in range(pieces):
                normalise(u, i * N_TILES // pieces, N_TILES // pieces)

        def turn(u, n):
            zt = psy.tile([P, J_BANK, P], F32, name="zt", tag="bank")
            for jl in range(J_BANK):
                jt = J_BANK * n + jl
                nc.tensor.transpose(zt[:, jl, :], z_of[u][:, jt * P : (jt + 1) * P], ident_f[:])
            zt_of[(u, n)] = zt

        def gate(u, n):
            g, v, m = units[u]
            if u not in gate_of:
                gated = (spool if v == 0 else rpool).tile([P, J_TILES, P], F32, name="gated")
                gate_of[u] = gated
            for jl in range(J_BANK):
                jt = J_BANK * n + jl
                col = 64 * v + 16 * g + jt
                nc.scalar.activation(
                    out=gate_of[u][:, jt, :],
                    in_=zt_of[(u, n)][:, jl, :],
                    func=(ACT.Sigmoid if v == 0 else ACT.Relu),
                    scale=prm_t[:, col : col + 1],
                    bias=prm_t[:, col + 32 : col + 33],
                )

        def turn_and_gate(u, some):
            for n in some:
                turn(u, n)
            for n in some:
                gate(u, n)

        def multiply(u, n, banks=1):
            blocks = slice(J_BANK * n, J_BANK * (n + banks))
            nc.vector.tensor_tensor(
                out=gate_of[u][:, blocks, :],
                in0=gate_of[u][:, blocks, :],
                in1=gate_of[u - MASKS][:, blocks, :],
                op=ALU.mult,
            )

        def turn_back(g, n):
            back = psx.tile([P, J_BANK, P], F32, name="back", tag="bank")
            first = 2 * MASKS * g + MASKS
            for jl in range(J_BANK):
                for m in range(MASKS):
                    nc.tensor.matmul(
                        out=back[:, jl, :],
                        lhsT=gate_of[first + m][:, J_BANK * n + jl, :],
                        rhs=ident_f[:],
                        is_transpose=True,
                        start=(m == 0),
                        stop=(m == MASKS - 1),
                    )
            back_of[(g, n)] = back

        def store(g, n, by_vector):
            result = stage.tile([P, N_TILE], F32, name="result")
            if by_vector:
                nc.vector.tensor_copy(out=result[:], in_=back_of[(g, n)][:].rearrange("p j b -> p (j b)"))
            else:
                nc.scalar.copy(out=result[:], in_=back_of[(g, n)][:].rearrange("p j b -> p (j b)"))
            nc.sync.dma_start(out=out[:, g * H + n * N_TILE : g * H + (n + 1) * N_TILE], in_=result[:])

        def keep_warm(passes):
            idle = psx.tile([P, N_TILE], F32, name="idle", tag="bank")
            for i in range(passes):
                nc.tensor.matmul(out=idle[:], lhsT=ident_b[:], rhs=x_sb[:, 0:N_TILE], start=True, stop=True)

        weigh(0, True)
        finish_mask(1)
        previous = None
        for gp in range(1, GROUPS * PASSES):
            grouped = weigh(gp, False)
            if previous is not None:
                quantise(gp - 1, previous)
            previous = grouped
        quantise(GROUPS * PASSES - 1, previous)

        open_banks(0, psx)
        open_banks(1, psy)
        for c in range(PASSES):
            chunk_passes(0, c)
            chunk_passes(1, c)
        for c in range(PASSES):
            load_half(1, 1, c // 2, c % 2)
        leave_psum(0)
        prm_ps = psx.tile([P, P], BF16, tag="bank")
        nc.tensor.transpose(prm_ps[:], prm[:], ident_b[:])
        prm_t = keep.tile([P, P], F32)
        nc.scalar.copy(out=prm_t[:], in_=prm_ps[:])
        leave_psum(1)
        for n in range(N_TILES):
            bank_stats(0, n)
        row_stats(0)
        bank_stats(1, 0)
        bank_stats(1, 1)
        finish_rows(0, 1)
        bank_stats(1, 2)
        bank_stats(1, 3)
        row_stats(1)
        finish_rows(1, 1)

        for n in range(N_TILES):
            for u in (2, 3):
                one_bank(u, n)
                leave_bank(u, n)
                bank_stats(u, n)
            if n >= 2:
                turn_and_gate(n - 2, ORDER)
        row_stats(2)
        row_stats(3)
        finish_rows(2, 1)
        finish_rows(3, 1)

        open_banks(4, psx)
        for c in range(PASSES):
            chunk_passes(4, c)
        leave_psum(4)
        turn_and_gate(2, ORDER)
        for n in range(N_TILES):
            bank_stats(4, n)
        row_stats(4)
        finish_rows(4, 1)

        for n in range(N_TILES):
            one_bank(5, n)
            leave_bank(5, n)
            if n == 1:
                turn_and_gate(3, ORDER)
        turn_and_gate(4, ORDER)
        bank_stats(5, 0)
        multiply(2, 0, 2)
        bank_stats(5, 1)
        multiply(2, 2, 2)
        bank_stats(5, 2)
        bank_stats(5, 3)
        row_stats(5)
        finish_rows(5, 1)

        bank_by_bank(6)
        leave_psum(6)
        turn_and_gate(5, ORDER)
        bank_stats(6, 0)
        multiply(3, 0, 2)
        bank_stats(6, 1)
        multiply(3, 2, 2)
        bank_stats(6, 2)
        bank_stats(6, 3)
        row_stats(6)
        finish_rows(6, 1)

        bank_by_bank(7)
        leave_psum(7)
        turn_and_gate(6, ORDER)
        keep_warm(2)
        for n in range(N_TILES):
            turn_back(0, n)
            store(0, n, False)
            if n == 1:
                keep_warm(2)
        for n in range(N_TILES):
            bank_stats(7, n)
        row_stats(7)
        finish_rows(7, N_TILES)
        multiply(6, 0, 2)
        multiply(6, 2, 2)
        turn_and_gate(7, ORDER)
        keep_warm(3)
        for n in ORDER:
            multiply(7, n)
            turn_back(1, n)
            store(1, n, False)
